import numpy as np
import ml_dtypes


def mxq(x, axis, fmt="e4m3"):
    dtype, down = {"e4m3": (ml_dtypes.float8_e4m3fn, 7), "e5m2": (ml_dtypes.float8_e5m2, 14)}[fmt]
    v = np.moveaxis(np.asarray(x, np.float32).astype(ml_dtypes.bfloat16).astype(np.float64), axis, -1)
    blocks = v.reshape(v.shape[:-1] + (-1, 32))
    amax = np.abs(blocks).max(-1, keepdims=True)
    byte = np.maximum(np.where(amax > 0, np.frexp(amax)[1] - 1 + 127, 0) - down, 1)
    scale = np.exp2(byte - 127.0)
    codes = (blocks / scale).astype(np.float32).astype(dtype).astype(np.float64)
    return np.moveaxis((codes * scale).reshape(v.shape), -1, axis)


WIDE = False


def mx_kscale(k):
    if not WIDE:
        return np.ones(k)
    levels = np.array([10, -10, 5, -5, 0])
    if k % 512:
        return np.exp2(np.random.permutation(np.resize(levels, k // 32))).repeat(32)
    a = np.empty((k // 512, 16))
    for p in range(k // 512):
        a[p, :8] = np.random.permutation(np.resize(levels, 8))
        for g in range(8):
            far = levels[np.abs(levels - a[p, g]) >= 10]
            a[p, g + 8] = far[np.random.randint(len(far))]
    return np.exp2(a.ravel()).repeat(32)


BF16 = ml_dtypes.bfloat16


def bf(x):
    return np.asarray(x, np.float32).astype(BF16)


def f64(x):
    return np.asarray(x).astype(np.float64)


B, T, U, D_ENC, D_PRED, D_JOINT, VOCAB = 4, 64, 32, 512, 512, 512, 1024
LOGIT_CLAMP = 15.0


def setup_inputs():
    se, sp = mx_kscale(D_ENC), mx_kscale(D_PRED)
    t = mx_kscale(D_JOINT)
    g = t / t.max()
    return {"encoder_out": bf(np.random.standard_normal((B, T, D_ENC)) * se),
            "predictor_out": bf(np.random.standard_normal((B, U, D_PRED)) * sp),
            "W_enc": bf(np.random.standard_normal((D_ENC, D_JOINT)) * 0.7 / np.sqrt(D_ENC) / se[:, None] * g),
            "b_enc": bf(np.random.standard_normal(D_JOINT) * 0.2 * g),
            "W_pred": bf(np.random.standard_normal((D_PRED, D_JOINT)) * 0.7 / np.sqrt(D_PRED) / sp[:, None] * g),
            "b_pred": bf(np.random.standard_normal(D_JOINT) * 0.2 * g),
            "W_out": bf(np.random.standard_normal((D_JOINT, VOCAB)) * 8.0 / np.sqrt(D_JOINT) / g[:, None]),
            "b_out": bf(np.random.standard_normal(VOCAB) * 0.5)}


def reference(encoder_out, predictor_out, W_enc, b_enc, W_pred, b_pred, W_out, b_out):
    enc = (mxq(f64(encoder_out), 2, "e4m3") @ mxq(f64(W_enc), 0, "e4m3")) + f64(b_enc)
    pred = (mxq(f64(predictor_out), 2, "e4m3") @ mxq(f64(W_pred), 0, "e4m3")) + f64(b_pred)
    joint = np.tanh(enc[:, :, None, :] + pred[:, None, :, :])
    logits = (mxq(joint, 3, "e4m3") @ mxq(f64(W_out), 0, "e4m3")) + f64(b_out)
    return np.clip(logits, -LOGIT_CLAMP, LOGIT_CLAMP)

@@ -1,0 +1,291 @@
+import concourse.mybir as mybir
+from concourse.masks import make_identity
+
+F32 = mybir.dt.float32
+BF16 = mybir.dt.bfloat16
+U32 = mybir.dt.uint32
+U8 = mybir.dt.uint8
+FP8X4 = mybir.dt.float8_e4m3fn_x4
+ADD = mybir.AluOpType.add
+MIN = mybir.AluOpType.min
+MAX = mybir.AluOpType.max
+TANH = mybir.ActivationFunctionType.Tanh
+IDENTITY = mybir.ActivationFunctionType.Identity
+
+P = 128
+PACK = 4
+BATCH, T_LEN, U_LEN = 4, 64, 32
+DIM = P * PACK
+VOCAB = 1024
+BANK = 512
+LOGIT_CLAMP = 15.0
+
+ENC_TOKENS = BATCH * T_LEN
+PRED_TOKENS = BATCH * U_LEN
+TOKEN_TILES = (ENC_TOKENS + PRED_TOKENS) // P
+T_STEP = 16
+ROUND_ROWS = T_STEP * U_LEN
+ROUNDS = BATCH * T_LEN // T_STEP
+ROW_TILES = ROUND_ROWS // P
+VOCAB_BLOCKS = VOCAB // P
+BLOCKS_IN_BANK = BANK // P
+VOCAB_HALVES = VOCAB // BANK
+HALF_OF_PSUM = 4
+T_ON_VECTOR = 12
+
+FLOPS = 2 * DIM * (ENC_TOKENS * DIM + PRED_TOKENS * DIM + BATCH * T_LEN * U_LEN * VOCAB)
+
+
+def load_k_first(nc, pool, weight, width, name):
+    raw = pool.tile([P, PACK, width], BF16, name=name)
+    nc.sync.dma_start(out=raw[:], in_=weight.rearrange("(p t) c -> p t c", t=PACK))
+    return raw
+
+
+def quantise(nc, grouped, codes, scales):
+    nc.vector.quantize_mx(
+        out=codes.bitcast(FP8X4),
+        scales=scales,
+        in_=grouped.rearrange("p c t -> p (c t)"),
+    )
+
+
+def tile_jointnetwork_kernel(
+    tc, encoder_out, predictor_out, W_enc, b_enc, W_pred, b_pred, W_out, b_out, out
+):
+    nc = tc.nc
+    out_rows = out.flatten_outer_dims()
+
+    with tc.tile_pool(name="keep", bufs=1) as keep:
+        tokens = keep.tile([P, TOKEN_TILES, DIM], BF16)
+        nc.sync.dma_start(
+            out=tokens[:, 0:2, :],
+            in_=encoder_out.flatten_outer_dims().rearrange("(n p) k -> p n k", p=P),
+        )
+        nc.sync.dma_start(out=tokens[:, 2, :], in_=predictor_out.flatten_outer_dims())
+        w_enc_raw = load_k_first(nc, keep, W_enc, DIM, "w_enc_raw")
+        w_pred_raw = load_k_first(nc, keep, W_pred, DIM, "w_pred_raw")
+        b_enc_columns = keep.tile([P, PACK], BF16)
+        nc.scalar.dma_start(out=b_enc_columns[:], in_=b_enc.rearrange("(p j) -> p j", j=PACK))
+        b_pred_columns = keep.tile([P, PACK], BF16)
+        nc.scalar.dma_start(out=b_pred_columns[:], in_=b_pred.rearrange("(p j) -> p j", j=PACK))
+        bias_rows = keep.tile([P, P], BF16)
+        nc.vector.memset(bias_rows[:], 0.0)
+        nc.scalar.dma_start(
+            out=bias_rows[0:VOCAB_BLOCKS, :], in_=b_out.rearrange("(c p) -> c p", p=P)
+        )
+        w_out_raw = load_k_first(nc, keep, W_out, VOCAB, "w_out_raw")
+
+        identity_bf16 = keep.tile([P, P], BF16)
+        make_identity(nc, identity_bf16[:])
+        identity_f32 = keep.tile([P, P], F32)
+        make_identity(nc, identity_f32[:])
+
+        token_codes = keep.tile([P, TOKEN_TILES * P], U32, align_bytes=64)
+        token_scales = keep.tile([P, TOKEN_TILES * P], U8, align_bytes=64)
+        w_enc_codes = keep.tile([P, DIM], U32, align_bytes=64)
+        w_enc_scales = keep.tile([P, DIM], U8, align_bytes=64)
+        w_pred_codes = keep.tile([P, DIM], U32, align_bytes=64)
+        w_pred_scales = keep.tile([P, DIM], U8, align_bytes=64)
+        w_out_codes = keep.tile([P, VOCAB], U32, align_bytes=64)
+        w_out_scales = keep.tile([P, VOCAB], U8, align_bytes=64)
+        projected = keep.tile([P, TOKEN_TILES * P, PACK], F32)
+        b_out_columns = keep.tile([P, VOCAB_BLOCKS], F32)
+
+        with tc.psum_pool(name="first_psum", bufs=2) as first_psum:
+            token_grouped = keep.tile([P, TOKEN_TILES * P, PACK], BF16, align_bytes=64)
+            for n in range(TOKEN_TILES):
+                flipped = first_psum.tile([P, 2, P], F32)
+                words = tokens[:, n, :].bitcast(F32)
+                for u in range(2):
+                    nc.tensor.transpose(flipped[:, u, :], words[:, u::2], identity_f32[:])
+                nc.scalar.copy(
+                    out=token_grouped[:, n * P : (n + 1) * P, :]
+                    .rearrange("p r t -> p (r t)")
+                    .bitcast(F32)
+                    .rearrange("p (r u) -> p r u", u=2),
+                    in_=flipped[:].rearrange("p u r -> p r u"),
+                )
+            bias_flipped = first_psum.tile([P, P], BF16)
+            nc.tensor.transpose(bias_flipped[:], bias_rows[:], identity_bf16[:])
+            nc.scalar.copy(out=b_out_columns[:], in_=bias_flipped[:, 0:VOCAB_BLOCKS])
+
+            w_enc_grouped = keep.tile([P, DIM, PACK], BF16, align_bytes=64)
+            nc.vector.tensor_copy(
+                out=w_enc_grouped[:].rearrange("p (j m) t -> p j m t", j=PACK),
+                in_=w_enc_raw[:].rearrange("p t (m j) -> p j m t", j=PACK),
+            )
+            w_pred_grouped = keep.tile([P, DIM, PACK], BF16, align_bytes=64)
+            nc.vector.tensor_copy(
+                out=w_pred_grouped[:].rearrange("p (j m) t -> p j m t", j=PACK),
+                in_=w_pred_raw[:].rearrange("p t (m j) -> p j m t", j=PACK),
+            )
+            quantise(
+                nc,
+                token_grouped[:, 0:ENC_TOKENS, :],
+                token_codes[:, 0:ENC_TOKENS],
+                token_scales[:, 0:ENC_TOKENS],
+            )
+            quantise(
+                nc,
+                token_grouped[:, ENC_TOKENS:, :],
+                token_codes[:, ENC_TOKENS:],
+                token_scales[:, ENC_TOKENS:],
+            )
+            quantise(nc, w_enc_grouped[:], w_enc_codes[:], w_enc_scales[:])
+            quantise(nc, w_pred_grouped[:], w_pred_codes[:], w_pred_scales[:])
+
+            for n in range(TOKEN_TILES):
+                is_encoder = n * P < ENC_TOKENS
+                codes = w_enc_codes if is_encoder else w_pred_codes
+                scales = w_enc_scales if is_encoder else w_pred_scales
+                bias = b_enc_columns if is_encoder else b_pred_columns
+                product = first_psum.tile([P, PACK, P], F32)
+                for j in range(PACK):
+                    nc.tensor.matmul_mx(
+                        out=product[:, j, :],
+                        lhsT=codes[:, j * P : (j + 1) * P].bitcast(FP8X4),
+                        lhsT_scale=scales[:, j * P : (j + 1) * P],
+                        rhs=token_codes[:, n * P : (n + 1) * P].bitcast(FP8X4),
+                        rhs_scale=token_scales[:, n * P : (n + 1) * P],
+                        start=True,
+                        stop=True,
+                    )
+                nc.vector.tensor_tensor(
+                    out=projected[:, n * P : (n + 1) * P, :],
+                    in0=product[:].rearrange("p j r -> p r j"),
+                    in1=bias[:].unsqueeze(1).to_broadcast([P, P, PACK]),
+                    op=ADD,
+                )
+
+            w_out_grouped = keep.tile([P, VOCAB, PACK], BF16, align_bytes=64)
+            nc.vector.tensor_copy(
+                out=w_out_grouped[:], in_=w_out_raw[:].rearrange("p t c -> p c t")
+            )
+            quantise(nc, w_out_grouped[:], w_out_codes[:], w_out_scales[:])
+
+        with (
+            tc.tile_pool(name="work", bufs=3) as work,
+            tc.tile_pool(name="wide", bufs=3) as wide,
+            tc.psum_pool(name="psum", bufs=HALF_OF_PSUM) as psum,
+        ):
+            summed_of = {}
+            joint_of = {}
+            codes_of = {}
+            biased_of = {}
+            logits_of = {}
+
+            def form_sum(r):
+                b = r * T_STEP // T_LEN
+                enc_first = r * T_STEP
+                pred_first = ENC_TOKENS + b * U_LEN
+                summed_of[r] = work.tile([P, T_STEP, U_LEN, PACK], F32, name="summed")
+                for engine, first, last in (
+                    (nc.vector, 0, T_ON_VECTOR),
+                    (nc.gpsimd, T_ON_VECTOR, T_STEP),
+                ):
+                    shape = [P, last - first, U_LEN, PACK]
+                    engine.tensor_tensor(
+                        out=summed_of[r][:, first:last, :, :],
+                        in0=projected[:, enc_first + first : enc_first + last, :]
+                        .unsqueeze(2)
+                        .to_broadcast(shape),
+                        in1=projected[:, pred_first : pred_first + U_LEN, :]
+                        .unsqueeze(1)
+                        .to_broadcast(shape),
+                        op=ADD,
+                    )
+
+            def take_tanh(r):
+                joint_of[r] = work.tile([P, ROUND_ROWS, PACK], BF16, align_bytes=64, name="joint")
+                nc.scalar.activation(
+                    out=joint_of[r][:],
+                    in_=summed_of[r][:].rearrange("p t u j -> p (t u) j"),
+                    func=TANH,
+                )
+
+            def quantise_joint(r):
+                codes = work.tile([P, ROUND_ROWS], U32, align_bytes=64, name="joint_codes")
+                scales = work.tile([P, ROUND_ROWS], U8, align_bytes=64, name="joint_scales")
+                quantise(nc, joint_of[r][:], codes[:], scales[:])
+                codes_of[r] = (codes, scales)
+
+            def project(r, half):
+                if half == 0:
+                    biased_of[r] = wide.tile([P, VOCAB_BLOCKS, ROUND_ROWS], F32, name="biased")
+                codes, scales = codes_of[r]
+                blocks = range(half * BLOCKS_IN_BANK, (half + 1) * BLOCKS_IN_BANK)
+                products = {}
+                for c in blocks:
+                    products[c] = psum.tile([P, ROUND_ROWS], F32, name="product")
+                    nc.tensor.matmul_mx(
+                        out=products[c][:],
+                        lhsT=w_out_codes[:, c * P : (c + 1) * P].bitcast(FP8X4),
+                        lhsT_scale=w_out_scales[:, c * P : (c + 1) * P],
+                        rhs=codes[:].bitcast(FP8X4),
+                        rhs_scale=scales[:],
+                        start=True,
+                        stop=True,
+                    )
+                for c in blocks:
+                    nc.scalar.activation(
+                        out=biased_of[r][:, c, :],
+                        in_=products[c][:],
+                        func=IDENTITY,
+                        bias=b_out_columns[:, c : c + 1],
+                    )
+
+            def turn_back(r, m):
+                turned = []
+                for h in range(VOCAB_HALVES):
+                    bank = psum.tile([P, BLOCKS_IN_BANK, P], F32, name="turned")
+                    for i in range(BLOCKS_IN_BANK):
+                        nc.tensor.transpose(
+                            bank[:, i, :],
+                            biased_of[r][:, h * BLOCKS_IN_BANK + i, m * P : (m + 1) * P],
+                            identity_f32[:],
+                        )
+                    turned.append(bank)
+                return turned
+
+            def clamp_and_store(r, m, turned):
+                if m == 0:
+                    logits_of[r] = wide.tile([P, ROW_TILES, VOCAB], F32, name="logits")
+                for h in range(VOCAB_HALVES):
+                    nc.vector.tensor_scalar(
+                        out=logits_of[r][:, m, h * BANK : (h + 1) * BANK],
+                        in0=turned[h][:].rearrange("p i v -> p (i v)"),
+                        scalar1=LOGIT_CLAMP,
+                        scalar2=-LOGIT_CLAMP,
+                        op0=MIN,
+                        op1=MAX,
+                    )
+                first_row = r * ROUND_ROWS + m * P
+                nc.sync.dma_start(
+                    out=out_rows[first_row : first_row + P, :], in_=logits_of[r][:, m, :]
+                )
+
+            with tc.manual_schedule():
+                for r in range(3):
+                    form_sum(r)
+                    take_tanh(r)
+                quantise_joint(0)
+                quantise_joint(1)
+                project(0, 0)
+                project(0, 1)
+                for r in range(ROUNDS):
+                    if r + 3 < ROUNDS:
+                        form_sum(r + 3)
+                    if r + 2 < ROUNDS:
+                        quantise_joint(r + 2)
+                    for half in range(VOCAB_HALVES):
+                        if r + 1 < ROUNDS:
+                            project(r + 1, half)
+                        if half == 0 and r + 3 < ROUNDS:
+                            take_tanh(r + 3)
+                        row_tiles = range(half * 2, half * 2 + 2)
+                        turned_of = {}
+                        for m in row_tiles:
+                            turned_of[m] = turn_back(r, m)
+                        for m in row_tiles:
+                            clamp_and_store(r, m, turned_of[m])

@@ -10,7 +10,6 @@ ADD = mybir.AluOpType.add
 MIN = mybir.AluOpType.min
 MAX = mybir.AluOpType.max
 TANH = mybir.ActivationFunctionType.Tanh
-IDENTITY = mybir.ActivationFunctionType.Identity
 
 P = 128
 PACK = 4
@@ -18,274 +17,319 @@ BATCH, T_LEN, U_LEN = 4, 64, 32
 DIM = P * PACK
 VOCAB = 1024
 BANK = 512
+VOCAB_HALVES = VOCAB // BANK
 LOGIT_CLAMP = 15.0
 
 ENC_TOKENS = BATCH * T_LEN
 PRED_TOKENS = BATCH * U_LEN
-TOKEN_TILES = (ENC_TOKENS + PRED_TOKENS) // P
-T_STEP = 16
-ROUND_ROWS = T_STEP * U_LEN
-ROUNDS = BATCH * T_LEN // T_STEP
-ROW_TILES = ROUND_ROWS // P
-VOCAB_BLOCKS = VOCAB // P
-BLOCKS_IN_BANK = BANK // P
-VOCAB_HALVES = VOCAB // BANK
-HALF_OF_PSUM = 4
-T_ON_VECTOR = 12
+TOKENS = ENC_TOKENS + PRED_TOKENS
+TOKEN_TILES = TOKENS // P
+
+LABELS_IN_TILE = 2
+LABEL_STEP = U_LEN // LABELS_IN_TILE
+ROW_TILES = 4
+ROUND_ROWS = ROW_TILES * P
+ROUNDS_IN_BATCH = LABEL_STEP // ROW_TILES
+ROUNDS = BATCH * ROUNDS_IN_BATCH
+SLICES = LABELS_IN_TILE * PACK
+RUN = 4
 
 FLOPS = 2 * DIM * (ENC_TOKENS * DIM + PRED_TOKENS * DIM + BATCH * T_LEN * U_LEN * VOCAB)
 
 
-def load_k_first(nc, pool, weight, width, name):
-    raw = pool.tile([P, PACK, width], BF16, name=name)
-    nc.sync.dma_start(out=raw[:], in_=weight.rearrange("(p t) c -> p t c", t=PACK))
-    return raw
-
-
 def quantise(nc, grouped, codes, scales):
-    nc.vector.quantize_mx(
-        out=codes.bitcast(FP8X4),
-        scales=scales,
-        in_=grouped.rearrange("p c t -> p (c t)"),
-    )
+    nc.vector.quantize_mx(out=codes.bitcast(FP8X4), scales=scales, in_=grouped)
 
 
 def tile_jointnetwork_kernel(
     tc, encoder_out, predictor_out, W_enc, b_enc, W_pred, b_pred, W_out, b_out, out
 ):
     nc = tc.nc
-    out_rows = out.flatten_outer_dims()
+    out_tiles = out.rearrange("b t (h u) v -> b (t h) u v", h=LABELS_IN_TILE)
 
-    with tc.tile_pool(name="keep", bufs=1) as keep:
+    with (
+        tc.tile_pool(name="keep", bufs=1) as keep,
+        tc.tile_pool(name="work", bufs=3) as work,
+        tc.tile_pool(name="rows", bufs=6) as rows,
+        tc.psum_pool(name="psum", bufs=8) as psum,
+        tc.manual_schedule(),
+    ):
+
+        def new_bank():
+            bank = psum.tile([P, BANK], F32, name="bank")
+            return bank
+
         tokens = keep.tile([P, TOKEN_TILES, DIM], BF16)
         nc.sync.dma_start(
             out=tokens[:, 0:2, :],
             in_=encoder_out.flatten_outer_dims().rearrange("(n p) k -> p n k", p=P),
         )
-        nc.sync.dma_start(out=tokens[:, 2, :], in_=predictor_out.flatten_outer_dims())
-        w_enc_raw = load_k_first(nc, keep, W_enc, DIM, "w_enc_raw")
-        w_pred_raw = load_k_first(nc, keep, W_pred, DIM, "w_pred_raw")
+        raw_of = {}
+        for name, weight, width in (("w_enc", W_enc, DIM), ("w_pred", W_pred, DIM)):
+            raw_of[name] = keep.tile([P, PACK, width], BF16, name=name + "_raw")
+            nc.sync.dma_start(
+                out=raw_of[name][:], in_=weight.rearrange("(p j) c -> p j c", j=PACK)
+            )
+            if name == "w_enc":
+                nc.sync.dma_start(
+                    out=tokens[:, 2, :], in_=predictor_out.flatten_outer_dims()
+                )
+        w_out_raw = keep.tile([P, PACK, VOCAB], BF16)
+        for half in range(VOCAB_HALVES):
+            cols = slice(half * BANK, (half + 1) * BANK)
+            nc.sync.dma_start(
+                out=w_out_raw[:, :, cols],
+                in_=W_out[:, cols].rearrange("(p j) c -> p j c", j=PACK),
+            )
+        b_out_rows = keep.tile([P, VOCAB], BF16)
+        nc.sync.dma_start(out=b_out_rows[:], in_=b_out.partition_broadcast(P))
         b_enc_columns = keep.tile([P, PACK], BF16)
         nc.scalar.dma_start(out=b_enc_columns[:], in_=b_enc.rearrange("(p j) -> p j", j=PACK))
         b_pred_columns = keep.tile([P, PACK], BF16)
         nc.scalar.dma_start(out=b_pred_columns[:], in_=b_pred.rearrange("(p j) -> p j", j=PACK))
-        bias_rows = keep.tile([P, P], BF16)
-        nc.vector.memset(bias_rows[:], 0.0)
-        nc.scalar.dma_start(
-            out=bias_rows[0:VOCAB_BLOCKS, :], in_=b_out.rearrange("(c p) -> c p", p=P)
-        )
-        w_out_raw = load_k_first(nc, keep, W_out, VOCAB, "w_out_raw")
 
-        identity_bf16 = keep.tile([P, P], BF16)
-        make_identity(nc, identity_bf16[:])
-        identity_f32 = keep.tile([P, P], F32)
-        make_identity(nc, identity_f32[:])
+        identity = keep.tile([P, P], F32)
+        make_identity(nc, identity[:])
+        warm = keep.tile([P, 1], F32)
+        nc.vector.memset(warm[:], 0.0)
+        nc.scalar.activation(out=warm[:], in_=warm[:], func=TANH)
 
-        token_codes = keep.tile([P, TOKEN_TILES * P], U32, align_bytes=64)
-        token_scales = keep.tile([P, TOKEN_TILES * P], U8, align_bytes=64)
+        token_codes = keep.tile([P, TOKENS], U32, align_bytes=64)
+        token_scales = keep.tile([P, TOKENS], U8, align_bytes=64)
         w_enc_codes = keep.tile([P, DIM], U32, align_bytes=64)
         w_enc_scales = keep.tile([P, DIM], U8, align_bytes=64)
         w_pred_codes = keep.tile([P, DIM], U32, align_bytes=64)
         w_pred_scales = keep.tile([P, DIM], U8, align_bytes=64)
         w_out_codes = keep.tile([P, VOCAB], U32, align_bytes=64)
         w_out_scales = keep.tile([P, VOCAB], U8, align_bytes=64)
-        projected = keep.tile([P, TOKEN_TILES * P, PACK], F32)
-        b_out_columns = keep.tile([P, VOCAB_BLOCKS], F32)
+        enc = keep.tile([P, PACK, ENC_TOKENS], F32)
+        pred = keep.tile([P, PACK, PRED_TOKENS], F32)
 
-        with tc.psum_pool(name="first_psum", bufs=2) as first_psum:
-            token_grouped = keep.tile([P, TOKEN_TILES * P, PACK], BF16, align_bytes=64)
-            for n in range(TOKEN_TILES):
-                flipped = first_psum.tile([P, 2, P], F32)
-                words = tokens[:, n, :].bitcast(F32)
-                for u in range(2):
-                    nc.tensor.transpose(flipped[:, u, :], words[:, u::2], identity_f32[:])
-                nc.scalar.copy(
-                    out=token_grouped[:, n * P : (n + 1) * P, :]
-                    .rearrange("p r t -> p (r t)")
-                    .bitcast(F32)
-                    .rearrange("p (r u) -> p r u", u=2),
-                    in_=flipped[:].rearrange("p u r -> p r u"),
+        def group_projection(engine_copy, raw, name):
+            grouped = keep.tile([P, DIM * PACK], BF16, align_bytes=64, name=name)
+            engine_copy(
+                out=grouped[:].rearrange("p (t m j) -> p t m j", t=PACK, j=PACK),
+                in_=raw[:].rearrange("p j (m t) -> p t m j", t=PACK),
+            )
+            return grouped
+
+        token_grouped = keep.tile([P, TOKENS * PACK], BF16, align_bytes=64)
+
+        def group_tokens(n):
+            flipped = new_bank()
+            words = tokens[:, n, :].bitcast(F32)
+            for w in range(2):
+                nc.tensor.transpose(flipped[:, w * P : (w + 1) * P], words[:, w::2], identity[:])
+            nc.scalar.copy(
+                out=token_grouped[:, n * P * PACK : (n + 1) * P * PACK]
+                .bitcast(F32)
+                .rearrange("p (r w) -> p r w", w=2),
+                in_=flipped[:, 0 : 2 * P].rearrange("p (w r) -> p r w", w=2),
+            )
+
+        def quantise_tokens(first, last):
+            quantise(
+                nc,
+                token_grouped[:, first * PACK : last * PACK],
+                token_codes[:, first:last],
+                token_scales[:, first:last],
+            )
+
+        def project(out_cols, codes, scales, j, first, last):
+            nc.tensor.matmul_mx(
+                out=out_cols,
+                lhsT=codes[:, j * P : (j + 1) * P].bitcast(FP8X4),
+                lhsT_scale=scales[:, j * P : (j + 1) * P],
+                rhs=token_codes[:, first:last].bitcast(FP8X4),
+                rhs_scale=token_scales[:, first:last],
+                start=True,
+                stop=True,
+            )
+
+        w_enc_grouped = group_projection(nc.vector.tensor_copy, raw_of["w_enc"], "w_enc_grouped")
+        group_tokens(0)
+        group_tokens(1)
+        group_tokens(2)
+        w_pred_grouped = group_projection(nc.scalar.copy, raw_of["w_pred"], "w_pred_grouped")
+        quantise_tokens(0, ENC_TOKENS)
+        quantise(nc, w_enc_grouped[:], w_enc_codes[:], w_enc_scales[:])
+        quantise_tokens(ENC_TOKENS, TOKENS)
+
+        w_out_grouped = keep.tile([P, VOCAB, PACK], BF16, align_bytes=64)
+
+        def group_w_out(engine_copy, half):
+            cols = slice(half * BANK, (half + 1) * BANK)
+            engine_copy(
+                out=w_out_grouped[:, cols, :],
+                in_=w_out_raw[:, :, cols].rearrange("p j c -> p c j"),
+            )
+
+        enc_banks = []
+        for first_j in range(0, PACK, 2):
+            bank = new_bank()
+            for j in range(first_j, first_j + 2):
+                project(
+                    bank[:, (j - first_j) * ENC_TOKENS : (j - first_j + 1) * ENC_TOKENS],
+                    w_enc_codes, w_enc_scales, j, 0, ENC_TOKENS,
                 )
-            bias_flipped = first_psum.tile([P, P], BF16)
-            nc.tensor.transpose(bias_flipped[:], bias_rows[:], identity_bf16[:])
-            nc.scalar.copy(out=b_out_columns[:], in_=bias_flipped[:, 0:VOCAB_BLOCKS])
+            enc_banks.append(bank)
+        group_w_out(nc.vector.tensor_copy, 0)
+        quantise(nc, w_pred_grouped[:], w_pred_codes[:], w_pred_scales[:])
+        pred_bank = new_bank()
+        for j in range(PACK):
+            project(
+                pred_bank[:, j * P : (j + 1) * P],
+                w_pred_codes, w_pred_scales, j, ENC_TOKENS, TOKENS,
+            )
+        for first_j in range(0, PACK, 2):
+            nc.vector.tensor_tensor(
+                out=enc[:, first_j : first_j + 2, :],
+                in0=enc_banks[first_j // 2][:].rearrange("p (j r) -> p j r", j=2),
+                in1=b_enc_columns[:, first_j : first_j + 2]
+                .unsqueeze(2)
+                .to_broadcast([P, 2, ENC_TOKENS]),
+                op=ADD,
+            )
+        nc.vector.tensor_tensor(
+            out=pred[:],
+            in0=pred_bank[:].rearrange("p (j r) -> p j r", j=PACK),
+            in1=b_pred_columns[:].unsqueeze(2).to_broadcast([P, PACK, PRED_TOKENS]),
+            op=ADD,
+        )
+        group_w_out(nc.scalar.copy, 1)
 
-            w_enc_grouped = keep.tile([P, DIM, PACK], BF16, align_bytes=64)
-            nc.vector.tensor_copy(
-                out=w_enc_grouped[:].rearrange("p (j m) t -> p j m t", j=PACK),
-                in_=w_enc_raw[:].rearrange("p t (m j) -> p j m t", j=PACK),
-            )
-            w_pred_grouped = keep.tile([P, DIM, PACK], BF16, align_bytes=64)
-            nc.vector.tensor_copy(
-                out=w_pred_grouped[:].rearrange("p (j m) t -> p j m t", j=PACK),
-                in_=w_pred_raw[:].rearrange("p t (m j) -> p j m t", j=PACK),
-            )
-            quantise(
-                nc,
-                token_grouped[:, 0:ENC_TOKENS, :],
-                token_codes[:, 0:ENC_TOKENS],
-                token_scales[:, 0:ENC_TOKENS],
-            )
-            quantise(
-                nc,
-                token_grouped[:, ENC_TOKENS:, :],
-                token_codes[:, ENC_TOKENS:],
-                token_scales[:, ENC_TOKENS:],
-            )
-            quantise(nc, w_enc_grouped[:], w_enc_codes[:], w_enc_scales[:])
-            quantise(nc, w_pred_grouped[:], w_pred_codes[:], w_pred_scales[:])
+        joint_of = {}
+        grouped_of = {}
+        codes_of = {}
+        biased_of = {}
+        banks_of = {}
 
-            for n in range(TOKEN_TILES):
-                is_encoder = n * P < ENC_TOKENS
-                codes = w_enc_codes if is_encoder else w_pred_codes
-                scales = w_enc_scales if is_encoder else w_pred_scales
-                bias = b_enc_columns if is_encoder else b_pred_columns
-                product = first_psum.tile([P, PACK, P], F32)
+        def first_label(r, m):
+            return (r % ROUNDS_IN_BATCH) * ROW_TILES + m
+
+        def take_tanh(r, m):
+            b = r // ROUNDS_IN_BATCH
+            joint = work.tile([P, SLICES, T_LEN], BF16, align_bytes=64, name="joint%d" % m)
+            for h in range(LABELS_IN_TILE):
+                label = b * U_LEN + first_label(r, m) + h * LABEL_STEP
                 for j in range(PACK):
-                    nc.tensor.matmul_mx(
-                        out=product[:, j, :],
-                        lhsT=codes[:, j * P : (j + 1) * P].bitcast(FP8X4),
-                        lhsT_scale=scales[:, j * P : (j + 1) * P],
-                        rhs=token_codes[:, n * P : (n + 1) * P].bitcast(FP8X4),
-                        rhs_scale=token_scales[:, n * P : (n + 1) * P],
-                        start=True,
-                        stop=True,
+                    nc.scalar.activation(
+                        out=joint[:, h * PACK + j, :],
+                        in_=enc[:, j, b * T_LEN : (b + 1) * T_LEN],
+                        func=TANH,
+                        bias=pred[:, j, label : label + 1],
                     )
+            joint_of[r, m] = joint
+
+        def group_joint(engine_copy, r, m):
+            if r not in grouped_of:
+                grouped_of[r] = work.tile(
+                    [P, ROW_TILES, T_LEN, SLICES], BF16, align_bytes=64, name="grouped"
+                )
+            engine_copy(
+                out=grouped_of[r][:, m].rearrange("p (c i) q -> p c q i", i=RUN),
+                in_=joint_of[r, m][:].rearrange("p q (c i) -> p c q i", i=RUN),
+            )
+
+        def quantise_joint(r, first, last):
+            if r not in codes_of:
+                codes_of[r] = (
+                    work.tile([P, ROUND_ROWS], U32, align_bytes=64, name="joint_codes"),
+                    work.tile([P, ROUND_ROWS], U8, align_bytes=64, name="joint_scales"),
+                )
+            codes, scales = codes_of[r]
+            cols = slice(first * P, last * P)
+            quantise(
+                nc,
+                grouped_of[r][:, first:last].rearrange("p m t q -> p (m t q)"),
+                codes[:, cols],
+                scales[:, cols],
+            )
+
+        def multiply(r, m):
+            codes, scales = codes_of[r]
+            row_cols = slice(m * P, (m + 1) * P)
+            banks = []
+            for half in range(VOCAB_HALVES):
+                cols = slice(half * BANK, (half + 1) * BANK)
+                bank = new_bank()
+                nc.tensor.matmul_mx(
+                    out=bank[:],
+                    lhsT=codes[:, row_cols].bitcast(FP8X4),
+                    lhsT_scale=scales[:, row_cols],
+                    rhs=w_out_codes[:, cols].bitcast(FP8X4),
+                    rhs_scale=w_out_scales[:, cols],
+                    start=True,
+                    stop=True,
+                )
+                banks.append(bank)
+            banks_of[r, m] = banks
+
+        def add_bias(r, m):
+            biased = rows.tile([P, VOCAB], F32, name="biased")
+            for half in range(VOCAB_HALVES):
+                cols = slice(half * BANK, (half + 1) * BANK)
                 nc.vector.tensor_tensor(
-                    out=projected[:, n * P : (n + 1) * P, :],
-                    in0=product[:].rearrange("p j r -> p r j"),
-                    in1=bias[:].unsqueeze(1).to_broadcast([P, P, PACK]),
+                    out=biased[:, cols],
+                    in0=banks_of[r, m][half][:],
+                    in1=b_out_rows[:, cols],
                     op=ADD,
                 )
+            biased_of[r, m] = biased
 
-            w_out_grouped = keep.tile([P, VOCAB, PACK], BF16, align_bytes=64)
-            nc.vector.tensor_copy(
-                out=w_out_grouped[:], in_=w_out_raw[:].rearrange("p t c -> p c t")
+        def clamp_and_store(r, m):
+            logits = rows.tile([P, VOCAB], F32, name="logits")
+            for half in range(VOCAB_HALVES):
+                cols = slice(half * BANK, (half + 1) * BANK)
+                nc.gpsimd.tensor_scalar(
+                    out=logits[:, cols],
+                    in0=biased_of[r, m][:, cols],
+                    scalar1=LOGIT_CLAMP,
+                    scalar2=-LOGIT_CLAMP,
+                    op0=MIN,
+                    op1=MAX,
+                )
+            nc.sync.dma_start(
+                out=out_tiles[r // ROUNDS_IN_BATCH, :, first_label(r, m), :], in_=logits[:]
             )
-            quantise(nc, w_out_grouped[:], w_out_codes[:], w_out_scales[:])
 
-        with (
-            tc.tile_pool(name="work", bufs=3) as work,
-            tc.tile_pool(name="wide", bufs=3) as wide,
-            tc.psum_pool(name="psum", bufs=HALF_OF_PSUM) as psum,
-        ):
-            summed_of = {}
-            joint_of = {}
-            codes_of = {}
-            biased_of = {}
-            logits_of = {}
+        for m in range(ROW_TILES):
+            take_tanh(0, m)
+        quantise(
+            nc,
+            w_out_grouped[:, 0:BANK, :].rearrange("p c j -> p (c j)"),
+            w_out_codes[:, 0:BANK],
+            w_out_scales[:, 0:BANK],
+        )
+        quantise(
+            nc,
+            w_out_grouped[:, BANK:, :].rearrange("p c j -> p (c j)"),
+            w_out_codes[:, BANK:],
+            w_out_scales[:, BANK:],
+        )
+        for m in range(ROW_TILES):
+            group_joint(nc.vector.tensor_copy, 0, m)
+            quantise_joint(0, m, m + 1)
+            multiply(0, m)
+        for m in range(ROW_TILES):
+            take_tanh(1, m)
+        for m in range(ROW_TILES - 1):
+            group_joint(nc.scalar.copy, 1, m)
 
-            def form_sum(r):
-                b = r * T_STEP // T_LEN
-                enc_first = r * T_STEP
-                pred_first = ENC_TOKENS + b * U_LEN
-                summed_of[r] = work.tile([P, T_STEP, U_LEN, PACK], F32, name="summed")
-                for engine, first, last in (
-                    (nc.vector, 0, T_ON_VECTOR),
-                    (nc.gpsimd, T_ON_VECTOR, T_STEP),
-                ):
-                    shape = [P, last - first, U_LEN, PACK]
-                    engine.tensor_tensor(
-                        out=summed_of[r][:, first:last, :, :],
-                        in0=projected[:, enc_first + first : enc_first + last, :]
-                        .unsqueeze(2)
-                        .to_broadcast(shape),
-                        in1=projected[:, pred_first : pred_first + U_LEN, :]
-                        .unsqueeze(1)
-                        .to_broadcast(shape),
-                        op=ADD,
-                    )
-
-            def take_tanh(r):
-                joint_of[r] = work.tile([P, ROUND_ROWS, PACK], BF16, align_bytes=64, name="joint")
-                nc.scalar.activation(
-                    out=joint_of[r][:],
-                    in_=summed_of[r][:].rearrange("p t u j -> p (t u) j"),
-                    func=TANH,
-                )
-
-            def quantise_joint(r):
-                codes = work.tile([P, ROUND_ROWS], U32, align_bytes=64, name="joint_codes")
-                scales = work.tile([P, ROUND_ROWS], U8, align_bytes=64, name="joint_scales")
-                quantise(nc, joint_of[r][:], codes[:], scales[:])
-                codes_of[r] = (codes, scales)
-
-            def project(r, half):
-                if half == 0:
-                    biased_of[r] = wide.tile([P, VOCAB_BLOCKS, ROUND_ROWS], F32, name="biased")
-                codes, scales = codes_of[r]
-                blocks = range(half * BLOCKS_IN_BANK, (half + 1) * BLOCKS_IN_BANK)
-                products = {}
-                for c in blocks:
-                    products[c] = psum.tile([P, ROUND_ROWS], F32, name="product")
-                    nc.tensor.matmul_mx(
-                        out=products[c][:],
-                        lhsT=w_out_codes[:, c * P : (c + 1) * P].bitcast(FP8X4),
-                        lhsT_scale=w_out_scales[:, c * P : (c + 1) * P],
-                        rhs=codes[:].bitcast(FP8X4),
-                        rhs_scale=scales[:],
-                        start=True,
-                        stop=True,
-                    )
-                for c in blocks:
-                    nc.scalar.activation(
-                        out=biased_of[r][:, c, :],
-                        in_=products[c][:],
-                        func=IDENTITY,
-                        bias=b_out_columns[:, c : c + 1],
-                    )
-
-            def turn_back(r, m):
-                turned = []
-                for h in range(VOCAB_HALVES):
-                    bank = psum.tile([P, BLOCKS_IN_BANK, P], F32, name="turned")
-                    for i in range(BLOCKS_IN_BANK):
-                        nc.tensor.transpose(
-                            bank[:, i, :],
-                            biased_of[r][:, h * BLOCKS_IN_BANK + i, m * P : (m + 1) * P],
-                            identity_f32[:],
-                        )
-                    turned.append(bank)
-                return turned
-
-            def clamp_and_store(r, m, turned):
-                if m == 0:
-                    logits_of[r] = wide.tile([P, ROW_TILES, VOCAB], F32, name="logits")
-                for h in range(VOCAB_HALVES):
-                    nc.vector.tensor_scalar(
-                        out=logits_of[r][:, m, h * BANK : (h + 1) * BANK],
-                        in0=turned[h][:].rearrange("p i v -> p (i v)"),
-                        scalar1=LOGIT_CLAMP,
-                        scalar2=-LOGIT_CLAMP,
-                        op0=MIN,
-                        op1=MAX,
-                    )
-                first_row = r * ROUND_ROWS + m * P
-                nc.sync.dma_start(
-                    out=out_rows[first_row : first_row + P, :], in_=logits_of[r][:, m, :]
-                )
-
-            with tc.manual_schedule():
-                for r in range(3):
-                    form_sum(r)
-                    take_tanh(r)
-                quantise_joint(0)
-                quantise_joint(1)
-                project(0, 0)
-                project(0, 1)
-                for r in range(ROUNDS):
-                    if r + 3 < ROUNDS:
-                        form_sum(r + 3)
-                    if r + 2 < ROUNDS:
-                        quantise_joint(r + 2)
-                    for half in range(VOCAB_HALVES):
-                        if r + 1 < ROUNDS:
-                            project(r + 1, half)
-                        if half == 0 and r + 3 < ROUNDS:
-                            take_tanh(r + 3)
-                        row_tiles = range(half * 2, half * 2 + 2)
-                        turned_of = {}
-                        for m in row_tiles:
-                            turned_of[m] = turn_back(r, m)
-                        for m in row_tiles:
-                            clamp_and_store(r, m, turned_of[m])
+        for r in range(ROUNDS):
+            if r + 2 < ROUNDS:
+                for m in range(ROW_TILES):
+                    take_tanh(r + 2, m)
+                for m in range(ROW_TILES - 1):
+                    group_joint(nc.scalar.copy, r + 2, m)
+            for m in range(ROW_TILES):
+                add_bias(r, m)
+                clamp_and_store(r, m)
+                if r + 1 < ROUNDS:
+                    if m == 0:
+                        group_joint(nc.vector.tensor_copy, r + 1, ROW_TILES - 1)
+                    if m == 1:
+                        quantise_joint(r + 1, 0, ROW_TILES)
+            if r + 1 < ROUNDS:
+                for m in range(ROW_TILES):
+                    multiply(r + 1, m)

@@ -279,16 +279,14 @@ def tile_jointnetwork_kernel(
 
         def clamp_and_store(r, m):
             logits = rows.tile([P, VOCAB], F32, name="logits")
-            for half in range(VOCAB_HALVES):
-                cols = slice(half * BANK, (half + 1) * BANK)
-                nc.gpsimd.tensor_scalar(
-                    out=logits[:, cols],
-                    in0=biased_of[r, m][:, cols],
-                    scalar1=LOGIT_CLAMP,
-                    scalar2=-LOGIT_CLAMP,
-                    op0=MIN,
-                    op1=MAX,
-                )
+            nc.gpsimd.tensor_scalar(
+                out=logits[:],
+                in0=biased_of[r, m][:],
+                scalar1=LOGIT_CLAMP,
+                scalar2=-LOGIT_CLAMP,
+                op0=MIN,
+                op1=MAX,
+            )
             nc.sync.dma_start(
                 out=out_tiles[r // ROUNDS_IN_BATCH, :, first_label(r, m), :], in_=logits[:]
             )

@@ -32,6 +32,7 @@ ROUND_ROWS = ROW_TILES * P
 ROUNDS_IN_BATCH = LABEL_STEP // ROW_TILES
 ROUNDS = BATCH * ROUNDS_IN_BATCH
 SLICES = LABELS_IN_TILE * PACK
+PAIR = 2
 RUN = 4
 
 FLOPS = 2 * DIM * (ENC_TOKENS * DIM + PRED_TOKENS * DIM + BATCH * T_LEN * U_LEN * VOCAB)
@@ -50,7 +51,7 @@ def tile_jointnetwork_kernel(
     with (
         tc.tile_pool(name="keep", bufs=1) as keep,
         tc.tile_pool(name="work", bufs=3) as work,
-        tc.tile_pool(name="rows", bufs=6) as rows,
+        tc.tile_pool(name="rows", bufs=4) as rows,
         tc.psum_pool(name="psum", bufs=8) as psum,
         tc.manual_schedule(),
     ):
@@ -266,29 +267,30 @@ def tile_jointnetwork_kernel(
             banks_of[r, m] = banks
 
         def add_bias(r, m):
-            biased = rows.tile([P, VOCAB], F32, name="biased")
+            if m % PAIR == 0:
+                biased_of[r, m // PAIR] = rows.tile([P, PAIR, VOCAB], F32, name="biased")
             for half in range(VOCAB_HALVES):
                 cols = slice(half * BANK, (half + 1) * BANK)
                 nc.vector.tensor_tensor(
-                    out=biased[:, cols],
+                    out=biased_of[r, m // PAIR][:, m % PAIR, cols],
                     in0=banks_of[r, m][half][:],
                     in1=b_out_rows[:, cols],
                     op=ADD,
                 )
-            biased_of[r, m] = biased
 
-        def clamp_and_store(r, m):
-            logits = rows.tile([P, VOCAB], F32, name="logits")
+        def clamp_and_store(r, pair):
+            logits = rows.tile([P, PAIR, VOCAB], F32, name="logits")
             nc.gpsimd.tensor_scalar(
                 out=logits[:],
-                in0=biased_of[r, m][:],
+                in0=biased_of[r, pair][:],
                 scalar1=LOGIT_CLAMP,
                 scalar2=-LOGIT_CLAMP,
                 op0=MIN,
                 op1=MAX,
             )
+            label = first_label(r, pair * PAIR)
             nc.sync.dma_start(
-                out=out_tiles[r // ROUNDS_IN_BATCH, :, first_label(r, m), :], in_=logits[:]
+                out=out_tiles[r // ROUNDS_IN_BATCH, :, label : label + PAIR, :], in_=logits[:]
             )
 
         for m in range(ROW_TILES):
@@ -322,7 +324,8 @@ def tile_jointnetwork_kernel(
                     group_joint(nc.scalar.copy, r + 2, m)
             for m in range(ROW_TILES):
                 add_bias(r, m)
-                clamp_and_store(r, m)
+                if m % PAIR == PAIR - 1:
+                    clamp_and_store(r, m // PAIR)
                 if r + 1 < ROUNDS:
                     if m == 0:
                         group_joint(nc.vector.tensor_copy, r + 1, ROW_TILES - 1)

@@ -33,6 +33,7 @@ ROUNDS_IN_BATCH = LABEL_STEP // ROW_TILES
 ROUNDS = BATCH * ROUNDS_IN_BATCH
 SLICES = LABELS_IN_TILE * PACK
 PAIR = 2
+VECTOR_COPY_ROUNDS = 2
 RUN = 4
 
 FLOPS = 2 * DIM * (ENC_TOKENS * DIM + PRED_TOKENS * DIM + BATCH * T_LEN * U_LEN * VOCAB)
@@ -51,7 +52,7 @@ def tile_jointnetwork_kernel(
     with (
         tc.tile_pool(name="keep", bufs=1) as keep,
         tc.tile_pool(name="work", bufs=3) as work,
-        tc.tile_pool(name="rows", bufs=4) as rows,
+        tc.tile_pool(name="rows", bufs=6) as rows,
         tc.psum_pool(name="psum", bufs=8) as psum,
         tc.manual_schedule(),
     ):
@@ -202,7 +203,7 @@ def tile_jointnetwork_kernel(
         joint_of = {}
         grouped_of = {}
         codes_of = {}
-        biased_of = {}
+        logits_of = {}
         banks_of = {}
 
         def first_label(r, m):
@@ -268,69 +269,85 @@ def tile_jointnetwork_kernel(
 
         def add_bias(r, m):
             if m % PAIR == 0:
-                biased_of[r, m // PAIR] = rows.tile([P, PAIR, VOCAB], F32, name="biased")
+                logits_of[r, m // PAIR] = rows.tile([P, PAIR, VOCAB], F32, name="logits")
             for half in range(VOCAB_HALVES):
                 cols = slice(half * BANK, (half + 1) * BANK)
                 nc.vector.tensor_tensor(
-                    out=biased_of[r, m // PAIR][:, m % PAIR, cols],
+                    out=logits_of[r, m // PAIR][:, m % PAIR, cols],
                     in0=banks_of[r, m][half][:],
                     in1=b_out_rows[:, cols],
                     op=ADD,
                 )
 
-        def clamp_and_store(r, pair):
-            logits = rows.tile([P, PAIR, VOCAB], F32, name="logits")
-            nc.gpsimd.tensor_scalar(
-                out=logits[:],
-                in0=biased_of[r, pair][:],
+        def clamp_and_store(engine, r, m, count):
+            logits = logits_of[r, m // PAIR][:, m % PAIR : m % PAIR + count, :]
+            engine.tensor_scalar(
+                out=logits,
+                in0=logits,
                 scalar1=LOGIT_CLAMP,
                 scalar2=-LOGIT_CLAMP,
                 op0=MIN,
                 op1=MAX,
             )
-            label = first_label(r, pair * PAIR)
+            label = first_label(r, m)
             nc.sync.dma_start(
-                out=out_tiles[r // ROUNDS_IN_BATCH, :, label : label + PAIR, :], in_=logits[:]
+                out=out_tiles[r // ROUNDS_IN_BATCH, :, label : label + count, :], in_=logits
             )
 
-        for m in range(ROW_TILES):
-            take_tanh(0, m)
-        quantise(
-            nc,
-            w_out_grouped[:, 0:BANK, :].rearrange("p c j -> p (c j)"),
-            w_out_codes[:, 0:BANK],
-            w_out_scales[:, 0:BANK],
-        )
-        quantise(
-            nc,
-            w_out_grouped[:, BANK:, :].rearrange("p c j -> p (c j)"),
-            w_out_codes[:, BANK:],
-            w_out_scales[:, BANK:],
-        )
+        def form_joint(r):
+            copy = nc.vector.tensor_copy if r < VECTOR_COPY_ROUNDS else nc.scalar.copy
+            for m in range(ROW_TILES):
+                take_tanh(r, m)
+                if r >= VECTOR_COPY_ROUNDS and m > 0:
+                    group_joint(copy, r, m - 1)
+            if r >= VECTOR_COPY_ROUNDS:
+                group_joint(copy, r, ROW_TILES - 1)
+
+        form_joint(0)
+        for half in range(VOCAB_HALVES):
+            cols = slice(half * BANK, (half + 1) * BANK)
+            quantise(
+                nc,
+                w_out_grouped[:, cols, :].rearrange("p c j -> p (c j)"),
+                w_out_codes[:, cols],
+                w_out_scales[:, cols],
+            )
         for m in range(ROW_TILES):
             group_joint(nc.vector.tensor_copy, 0, m)
             quantise_joint(0, m, m + 1)
             multiply(0, m)
-        for m in range(ROW_TILES):
-            take_tanh(1, m)
-        for m in range(ROW_TILES - 1):
-            group_joint(nc.scalar.copy, 1, m)
+        form_joint(1)
 
+        last = ROUNDS - 1
         for r in range(ROUNDS):
             if r + 2 < ROUNDS:
-                for m in range(ROW_TILES):
-                    take_tanh(r + 2, m)
-                for m in range(ROW_TILES - 1):
-                    group_joint(nc.scalar.copy, r + 2, m)
-            for m in range(ROW_TILES):
-                add_bias(r, m)
-                if m % PAIR == PAIR - 1:
-                    clamp_and_store(r, m // PAIR)
-                if r + 1 < ROUNDS:
-                    if m == 0:
-                        group_joint(nc.vector.tensor_copy, r + 1, ROW_TILES - 1)
-                    if m == 1:
-                        quantise_joint(r + 1, 0, ROW_TILES)
-            if r + 1 < ROUNDS:
-                for m in range(ROW_TILES):
-                    multiply(r + 1, m)
+                form_joint(r + 2)
+            add_bias(r, 0)
+            if r == last:
+                clamp_and_store(nc.gpsimd, r, 0, 1)
+            add_bias(r, 1)
+            if r == last:
+                clamp_and_store(nc.gpsimd, r, 1, 1)
+            else:
+                if r + 1 < VECTOR_COPY_ROUNDS:
+                    for m in range(ROW_TILES):
+                        group_joint(nc.vector.tensor_copy, r + 1, m)
+                quantise_joint(r + 1, 0, ROW_TILES)
+                multiply(r + 1, 0)
+                multiply(r + 1, 1)
+            if r > 0 and r % 2 == 0:
+                clamp_and_store(nc.vector, r - 1, ROW_TILES - 1, 1)
+            if r < last:
+                clamp_and_store(nc.gpsimd, r, 0, PAIR)
+            add_bias(r, 2)
+            if r < last:
+                multiply(r + 1, 2)
+            if r % 2 == 1:
+                clamp_and_store(nc.gpsimd, r, 2, 1)
+            add_bias(r, 3)
+            if r < last:
+                multiply(r + 1, 3)
+            if r == last:
+                clamp_and_store(nc.vector, r, 3, 1)
+            elif r % 2 == 0:
+                clamp_and_store(nc.gpsimd, r, 2, PAIR)

@@ -33,6 +33,8 @@ ROUNDS_IN_BATCH = LABEL_STEP // ROW_TILES
 ROUNDS = BATCH * ROUNDS_IN_BATCH
 SLICES = LABELS_IN_TILE * PACK
 PAIR = 2
+TILES = ROUNDS * ROW_TILES
+LONE_TILES = 4
 VECTOR_COPY_ROUNDS = 2
 RUN = 4
 
@@ -52,7 +54,7 @@ def tile_jointnetwork_kernel(
     with (
         tc.tile_pool(name="keep", bufs=1) as keep,
         tc.tile_pool(name="work", bufs=3) as work,
-        tc.tile_pool(name="rows", bufs=6) as rows,
+        tc.tile_pool(name="rows", bufs=4) as rows,
         tc.psum_pool(name="psum", bufs=8) as psum,
         tc.manual_schedule(),
     ):
@@ -267,32 +269,47 @@ def tile_jointnetwork_kernel(
                 banks.append(bank)
             banks_of[r, m] = banks
 
-        def add_bias(r, m):
-            if m % PAIR == 0:
-                logits_of[r, m // PAIR] = rows.tile([P, PAIR, VOCAB], F32, name="logits")
+        units = [(0, PAIR)]
+        while units[-1][1] + ROW_TILES <= TILES - LONE_TILES:
+            units.append((units[-1][1], units[-1][1] + ROW_TILES))
+        units.append((units[-1][1], TILES - LONE_TILES))
+        units.extend((i, i + 1) for i in range(TILES - LONE_TILES, TILES))
+        unit_of = {i: unit for unit in units for i in range(unit[0], unit[1])}
+
+        def add_bias(i):
+            first, end = unit_of[i]
+            if i == first:
+                logits_of[first] = rows.tile(
+                    [P, end - first, VOCAB], F32, name="logits%d" % (end - first)
+                )
             for half in range(VOCAB_HALVES):
                 cols = slice(half * BANK, (half + 1) * BANK)
                 nc.vector.tensor_tensor(
-                    out=logits_of[r, m // PAIR][:, m % PAIR, cols],
-                    in0=banks_of[r, m][half][:],
+                    out=logits_of[first][:, i - first, cols],
+                    in0=banks_of[i // ROW_TILES, i % ROW_TILES][half][:],
                     in1=b_out_rows[:, cols],
                     op=ADD,
                 )
+            if i == end - 1:
+                clamp_and_store(nc.vector if i == TILES - 1 else nc.gpsimd, first, end)
 
-        def clamp_and_store(engine, r, m, count):
-            logits = logits_of[r, m // PAIR][:, m % PAIR : m % PAIR + count, :]
+        def clamp_and_store(engine, first, end):
+            logits = logits_of[first]
             engine.tensor_scalar(
-                out=logits,
-                in0=logits,
+                out=logits[:],
+                in0=logits[:],
                 scalar1=LOGIT_CLAMP,
                 scalar2=-LOGIT_CLAMP,
                 op0=MIN,
                 op1=MAX,
             )
-            label = first_label(r, m)
-            nc.sync.dma_start(
-                out=out_tiles[r // ROUNDS_IN_BATCH, :, label : label + count, :], in_=logits
-            )
+            for i in range(first, end, PAIR):
+                count = min(PAIR, end - i)
+                b, label = divmod(i, LABEL_STEP)
+                nc.sync.dma_start(
+                    out=out_tiles[b, :, label : label + count, :],
+                    in_=logits[:, i - first : i - first + count, :],
+                )
 
         def form_joint(r):
             copy = nc.vector.tensor_copy if r < VECTOR_COPY_ROUNDS else nc.scalar.copy
@@ -318,36 +335,18 @@ def tile_jointnetwork_kernel(
             multiply(0, m)
         form_joint(1)
 
-        last = ROUNDS - 1
         for r in range(ROUNDS):
+            more = r + 1 < ROUNDS
             if r + 2 < ROUNDS:
                 form_joint(r + 2)
-            add_bias(r, 0)
-            if r == last:
-                clamp_and_store(nc.gpsimd, r, 0, 1)
-            add_bias(r, 1)
-            if r == last:
-                clamp_and_store(nc.gpsimd, r, 1, 1)
-            else:
-                if r + 1 < VECTOR_COPY_ROUNDS:
-                    for m in range(ROW_TILES):
-                        group_joint(nc.vector.tensor_copy, r + 1, m)
-                quantise_joint(r + 1, 0, ROW_TILES)
-                multiply(r + 1, 0)
-                multiply(r + 1, 1)
-            if r > 0 and r % 2 == 0:
-                clamp_and_store(nc.vector, r - 1, ROW_TILES - 1, 1)
-            if r < last:
-                clamp_and_store(nc.gpsimd, r, 0, PAIR)
-            add_bias(r, 2)
-            if r < last:
-                multiply(r + 1, 2)
-            if r % 2 == 1:
-                clamp_and_store(nc.gpsimd, r, 2, 1)
-            add_bias(r, 3)
-            if r < last:
-                multiply(r + 1, 3)
-            if r == last:
-                clamp_and_store(nc.vector, r, 3, 1)
-            elif r % 2 == 0:
-                clamp_and_store(nc.gpsimd, r, 2, PAIR)
+            for m in range(ROW_TILES):
+                if m == PAIR and more:
+                    if r + 1 < VECTOR_COPY_ROUNDS:
+                        for n in range(ROW_TILES):
+                            group_joint(nc.vector.tensor_copy, r + 1, n)
+                    quantise_joint(r + 1, 0, ROW_TILES)
+                    multiply(r + 1, 0)
+                    multiply(r + 1, 1)
+                add_bias(r * ROW_TILES + m)
+                if m >= PAIR and more:
+                    multiply(r + 1, m)

@@ -34,7 +34,9 @@ ROUNDS = BATCH * ROUNDS_IN_BATCH
 SLICES = LABELS_IN_TILE * PACK
 PAIR = 2
 TILES = ROUNDS * ROW_TILES
-LONE_TILES = 4
+TILES_AHEAD = 3
+ADDED_TILE = 3
+VECTOR_UNITS = 2
 VECTOR_COPY_ROUNDS = 2
 RUN = 4
 
@@ -55,12 +57,17 @@ def tile_jointnetwork_kernel(
         tc.tile_pool(name="keep", bufs=1) as keep,
         tc.tile_pool(name="work", bufs=3) as work,
         tc.tile_pool(name="rows", bufs=4) as rows,
-        tc.psum_pool(name="psum", bufs=8) as psum,
+        tc.psum_pool(name="psum", bufs=2 * TILES_AHEAD) as psum,
+        tc.psum_pool(name="side_psum", bufs=2) as side_psum,
         tc.manual_schedule(),
     ):
 
         def new_bank():
             bank = psum.tile([P, BANK], F32, name="bank")
+            return bank
+
+        def new_side_bank():
+            bank = side_psum.tile([P, BANK], F32, name="side_bank")
             return bank
 
         tokens = keep.tile([P, TOKEN_TILES, DIM], BF16)
@@ -106,8 +113,20 @@ def tile_jointnetwork_kernel(
         w_pred_scales = keep.tile([P, DIM], U8, align_bytes=64)
         w_out_codes = keep.tile([P, VOCAB], U32, align_bytes=64)
         w_out_scales = keep.tile([P, VOCAB], U8, align_bytes=64)
-        enc = keep.tile([P, PACK, ENC_TOKENS], F32)
-        pred = keep.tile([P, PACK, PRED_TOKENS], F32)
+        sides = keep.tile([P, PACK, BATCH, P], F32)
+        nc.gpsimd.memset(sides[:, :, :, T_LEN + U_LEN :], 0.0)
+        adders = keep.tile([P, ROUNDS_IN_BATCH, T_LEN, LABELS_IN_TILE], F32)
+        for q in range(ROUNDS_IN_BATCH):
+            label = T_LEN + q * ROW_TILES + ADDED_TILE
+            shape = [P, T_LEN, LABELS_IN_TILE]
+            nc.gpsimd.tensor_tensor(
+                out=adders[:, q],
+                in0=identity[:, 0:T_LEN].unsqueeze(2).to_broadcast(shape),
+                in1=identity[:, label : label + LABEL_STEP + 1 : LABEL_STEP]
+                .unsqueeze(1)
+                .to_broadcast(shape),
+                op=ADD,
+            )
 
         def group_projection(engine_copy, raw, name):
             grouped = keep.tile([P, DIM * PACK], BF16, align_bytes=64, name=name)
@@ -120,7 +139,7 @@ def tile_jointnetwork_kernel(
         token_grouped = keep.tile([P, TOKENS * PACK], BF16, align_bytes=64)
 
         def group_tokens(n):
-            flipped = new_bank()
+            flipped = new_side_bank()
             words = tokens[:, n, :].bitcast(F32)
             for w in range(2):
                 nc.tensor.transpose(flipped[:, w * P : (w + 1) * P], words[:, w::2], identity[:])
@@ -187,23 +206,29 @@ def tile_jointnetwork_kernel(
             )
         for first_j in range(0, PACK, 2):
             nc.vector.tensor_tensor(
-                out=enc[:, first_j : first_j + 2, :],
-                in0=enc_banks[first_j // 2][:].rearrange("p (j r) -> p j r", j=2),
+                out=sides[:, first_j : first_j + 2, :, 0:T_LEN],
+                in0=enc_banks[first_j // 2][:].rearrange("p (j b t) -> p j b t", j=2, b=BATCH),
                 in1=b_enc_columns[:, first_j : first_j + 2]
                 .unsqueeze(2)
-                .to_broadcast([P, 2, ENC_TOKENS]),
+                .unsqueeze(3)
+                .to_broadcast([P, 2, BATCH, T_LEN]),
                 op=ADD,
             )
         nc.vector.tensor_tensor(
-            out=pred[:],
-            in0=pred_bank[:].rearrange("p (j r) -> p j r", j=PACK),
-            in1=b_pred_columns[:].unsqueeze(2).to_broadcast([P, PACK, PRED_TOKENS]),
+            out=sides[:, :, :, T_LEN : T_LEN + U_LEN],
+            in0=pred_bank[:].rearrange("p (j b u) -> p j b u", j=PACK, b=BATCH),
+            in1=b_pred_columns[:]
+            .unsqueeze(2)
+            .unsqueeze(3)
+            .to_broadcast([P, PACK, BATCH, U_LEN]),
             op=ADD,
         )
         group_w_out(nc.scalar.copy, 1)
 
         joint_of = {}
         grouped_of = {}
+        turned_of = {}
+        sum_of = {}
         codes_of = {}
         logits_of = {}
         banks_of = {}
@@ -215,21 +240,54 @@ def tile_jointnetwork_kernel(
             b = r // ROUNDS_IN_BATCH
             joint = work.tile([P, SLICES, T_LEN], BF16, align_bytes=64, name="joint%d" % m)
             for h in range(LABELS_IN_TILE):
-                label = b * U_LEN + first_label(r, m) + h * LABEL_STEP
+                label = T_LEN + first_label(r, m) + h * LABEL_STEP
                 for j in range(PACK):
                     nc.scalar.activation(
                         out=joint[:, h * PACK + j, :],
-                        in_=enc[:, j, b * T_LEN : (b + 1) * T_LEN],
+                        in_=sides[:, j, b, 0:T_LEN],
                         func=TANH,
-                        bias=pred[:, j, label : label + 1],
+                        bias=sides[:, j, b, label : label + 1],
                     )
             joint_of[r, m] = joint
 
-        def group_joint(engine_copy, r, m):
+        def new_grouped(r):
             if r not in grouped_of:
                 grouped_of[r] = work.tile(
                     [P, ROW_TILES, T_LEN, SLICES], BF16, align_bytes=64, name="grouped"
                 )
+
+        def turn_sides(b):
+            bank = new_side_bank()
+            for j in range(PACK):
+                cols = slice(j * P, (j + 1) * P)
+                nc.tensor.transpose(bank[:, cols], sides[:, j, b, :], identity[:])
+            turned_of[b] = keep.tile([P, DIM], F32, name="turned%d" % b)
+            nc.scalar.copy(out=turned_of[b][:], in_=bank[:])
+
+        def add_on_tensor(r):
+            b, q = divmod(r, ROUNDS_IN_BATCH)
+            bank = new_side_bank()
+            for j in range(PACK):
+                cols = slice(j * P, (j + 1) * P)
+                nc.tensor.matmul(
+                    bank[:, cols],
+                    lhsT=turned_of[b][:, cols],
+                    rhs=adders[:, q].rearrange("p t h -> p (t h)"),
+                    start=True,
+                    stop=True,
+                )
+            sum_of[r] = bank
+
+        def take_tanh_of_sum(r):
+            new_grouped(r)
+            nc.scalar.activation(
+                out=grouped_of[r][:, ADDED_TILE].rearrange("p t (h j) -> p (t h) j", j=PACK),
+                in_=sum_of[r][:].rearrange("p (j n) -> p n j", j=PACK),
+                func=TANH,
+            )
+
+        def group_joint(engine_copy, r, m):
+            new_grouped(r)
             engine_copy(
                 out=grouped_of[r][:, m].rearrange("p (c i) q -> p c q i", i=RUN),
                 in_=joint_of[r, m][:].rearrange("p q (c i) -> p c q i", i=RUN),
@@ -269,11 +327,13 @@ def tile_jointnetwork_kernel(
                 banks.append(bank)
             banks_of[r, m] = banks
 
-        units = [(0, PAIR)]
-        while units[-1][1] + ROW_TILES <= TILES - LONE_TILES:
-            units.append((units[-1][1], units[-1][1] + ROW_TILES))
-        units.append((units[-1][1], TILES - LONE_TILES))
-        units.extend((i, i + 1) for i in range(TILES - LONE_TILES, TILES))
+        first_sizes = [1, 1, PAIR, PAIR]
+        last_sizes = [PAIR, PAIR, PAIR, 1, PAIR, 1]
+        quads = (TILES - sum(first_sizes) - sum(last_sizes)) // ROW_TILES
+        units = []
+        for size in first_sizes + [ROW_TILES] * quads + last_sizes:
+            first = units[-1][1] if units else 0
+            units.append((first, first + size))
         unit_of = {i: unit for unit in units for i in range(unit[0], unit[1])}
 
         def add_bias(i):
@@ -290,8 +350,8 @@ def tile_jointnetwork_kernel(
                     in1=b_out_rows[:, cols],
                     op=ADD,
                 )
-            if i == end - 1:
-                clamp_and_store(nc.vector if i == TILES - 1 else nc.gpsimd, first, end)
+            if i == end - 1 and first < units[-VECTOR_UNITS][0]:
+                clamp_and_store(nc.gpsimd, first, end)
 
         def clamp_and_store(engine, first, end):
             logits = logits_of[first]
@@ -312,13 +372,17 @@ def tile_jointnetwork_kernel(
                 )
 
         def form_joint(r):
-            copy = nc.vector.tensor_copy if r < VECTOR_COPY_ROUNDS else nc.scalar.copy
-            for m in range(ROW_TILES):
-                take_tanh(r, m)
-                if r >= VECTOR_COPY_ROUNDS and m > 0:
-                    group_joint(copy, r, m - 1)
-            if r >= VECTOR_COPY_ROUNDS:
-                group_joint(copy, r, ROW_TILES - 1)
+            if r < VECTOR_COPY_ROUNDS:
+                for m in range(ROW_TILES):
+                    take_tanh(r, m)
+                return
+            take_tanh(r, 0)
+            take_tanh(r, 1)
+            group_joint(nc.scalar.copy, r, 0)
+            take_tanh(r, 2)
+            group_joint(nc.scalar.copy, r, 1)
+            take_tanh_of_sum(r)
+            group_joint(nc.scalar.copy, r, 2)
 
         form_joint(0)
         for half in range(VOCAB_HALVES):
@@ -332,21 +396,29 @@ def tile_jointnetwork_kernel(
         for m in range(ROW_TILES):
             group_joint(nc.vector.tensor_copy, 0, m)
             quantise_joint(0, m, m + 1)
-            multiply(0, m)
+            if m < TILES_AHEAD:
+                multiply(0, m)
         form_joint(1)
+        turn_sides(0)
+        add_on_tensor(VECTOR_COPY_ROUNDS)
 
         for r in range(ROUNDS):
-            more = r + 1 < ROUNDS
+            if r + 1 < BATCH:
+                turn_sides(r + 1)
             if r + 2 < ROUNDS:
                 form_joint(r + 2)
             for m in range(ROW_TILES):
-                if m == PAIR and more:
+                tile = r * ROW_TILES + m
+                add_bias(tile)
+                if m == PAIR - 1 and r + 1 < ROUNDS:
                     if r + 1 < VECTOR_COPY_ROUNDS:
                         for n in range(ROW_TILES):
                             group_joint(nc.vector.tensor_copy, r + 1, n)
                     quantise_joint(r + 1, 0, ROW_TILES)
-                    multiply(r + 1, 0)
-                    multiply(r + 1, 1)
-                add_bias(r * ROW_TILES + m)
-                if m >= PAIR and more:
-                    multiply(r + 1, m)
+                if tile + TILES_AHEAD < TILES:
+                    ahead = divmod(tile + TILES_AHEAD, ROW_TILES)
+                    multiply(ahead[0], ahead[1])
+            if r + 3 < ROUNDS:
+                add_on_tensor(r + 3)
+        for first, end in units[-VECTOR_UNITS:]:
+            clamp_and_store(nc.vector, first, end)

@@ -7,9 +7,11 @@ U32 = mybir.dt.uint32
 U8 = mybir.dt.uint8
 FP8X4 = mybir.dt.float8_e4m3fn_x4
 ADD = mybir.AluOpType.add
+MULT = mybir.AluOpType.mult
 MIN = mybir.AluOpType.min
 MAX = mybir.AluOpType.max
 TANH = mybir.ActivationFunctionType.Tanh
+IDENTITY = mybir.ActivationFunctionType.Identity
 
 P = 128
 PACK = 4
@@ -33,12 +35,23 @@ ROUNDS_IN_BATCH = LABEL_STEP // ROW_TILES
 ROUNDS = BATCH * ROUNDS_IN_BATCH
 SLICES = LABELS_IN_TILE * PACK
 PAIR = 2
+LOGITS_BUFS = {1: 2, 2: 6, 4: 3}
+LAST_PAIRS = 9
 TILES = ROUNDS * ROW_TILES
 TILES_AHEAD = 3
 ADDED_TILE = 3
-VECTOR_UNITS = 2
-VECTOR_COPY_ROUNDS = 2
+PLAIN_TILES = TILES - ROW_TILES
+VOCAB_BLOCKS = VOCAB // P
+BLOCKS_IN_BANK = BANK // P
 RUN = 4
+
+def first_label(r, m):
+    return (r % ROUNDS_IN_BATCH) * ROW_TILES + m
+
+
+def is_added(r, m):
+    return m == ADDED_TILE and r >= 2
+
 
 FLOPS = 2 * DIM * (ENC_TOKENS * DIM + PRED_TOKENS * DIM + BATCH * T_LEN * U_LEN * VOCAB)
 
@@ -56,7 +69,7 @@ def tile_jointnetwork_kernel(
     with (
         tc.tile_pool(name="keep", bufs=1) as keep,
         tc.tile_pool(name="work", bufs=3) as work,
-        tc.tile_pool(name="rows", bufs=4) as rows,
+        tc.tile_pool(name="rows", bufs=1) as rows,
         tc.psum_pool(name="psum", bufs=2 * TILES_AHEAD) as psum,
         tc.psum_pool(name="side_psum", bufs=2) as side_psum,
         tc.manual_schedule(),
@@ -104,6 +117,8 @@ def tile_jointnetwork_kernel(
         warm = keep.tile([P, 1], F32)
         nc.vector.memset(warm[:], 0.0)
         nc.scalar.activation(out=warm[:], in_=warm[:], func=TANH)
+        pick = keep.tile([P, 1], BF16)
+        nc.scalar.copy(out=pick[:], in_=identity[:, 0:1])
 
         token_codes = keep.tile([P, TOKENS], U32, align_bytes=64)
         token_scales = keep.tile([P, TOKENS], U8, align_bytes=64)
@@ -115,12 +130,15 @@ def tile_jointnetwork_kernel(
         w_out_scales = keep.tile([P, VOCAB], U8, align_bytes=64)
         sides = keep.tile([P, PACK, BATCH, P], F32)
         nc.gpsimd.memset(sides[:, :, :, T_LEN + U_LEN :], 0.0)
-        adders = keep.tile([P, ROUNDS_IN_BATCH, T_LEN, LABELS_IN_TILE], F32)
-        for q in range(ROUNDS_IN_BATCH):
-            label = T_LEN + q * ROW_TILES + ADDED_TILE
+        added_labels = sorted(
+            {first_label(r, m) for r in range(ROUNDS) for m in range(ROW_TILES) if is_added(r, m)}
+        )
+        adders = keep.tile([P, len(added_labels), T_LEN, LABELS_IN_TILE], F32)
+        for a, first in enumerate(added_labels):
+            label = T_LEN + first
             shape = [P, T_LEN, LABELS_IN_TILE]
             nc.gpsimd.tensor_tensor(
-                out=adders[:, q],
+                out=adders[:, a],
                 in0=identity[:, 0:T_LEN].unsqueeze(2).to_broadcast(shape),
                 in1=identity[:, label : label + LABEL_STEP + 1 : LABEL_STEP]
                 .unsqueeze(1)
@@ -173,18 +191,22 @@ def tile_jointnetwork_kernel(
         group_tokens(0)
         group_tokens(1)
         group_tokens(2)
-        w_pred_grouped = group_projection(nc.scalar.copy, raw_of["w_pred"], "w_pred_grouped")
         quantise_tokens(0, ENC_TOKENS)
         quantise(nc, w_enc_grouped[:], w_enc_codes[:], w_enc_scales[:])
+        w_pred_grouped = group_projection(nc.vector.tensor_copy, raw_of["w_pred"], "w_pred_grouped")
         quantise_tokens(ENC_TOKENS, TOKENS)
 
         w_out_grouped = keep.tile([P, VOCAB, PACK], BF16, align_bytes=64)
 
-        def group_w_out(engine_copy, half):
-            cols = slice(half * BANK, (half + 1) * BANK)
-            engine_copy(
+        for first in range(BANK, VOCAB, P):
+            cols = slice(first, first + P)
+            nc.gpsimd.tensor_scalar(
                 out=w_out_grouped[:, cols, :],
-                in_=w_out_raw[:, :, cols].rearrange("p j c -> p c j"),
+                in0=w_out_raw[:, :, cols].rearrange("p j c -> p c j"),
+                scalar1=1.0,
+                scalar2=0.0,
+                op0=MULT,
+                op1=ADD,
             )
 
         enc_banks = []
@@ -196,7 +218,20 @@ def tile_jointnetwork_kernel(
                     w_enc_codes, w_enc_scales, j, 0, ENC_TOKENS,
                 )
             enc_banks.append(bank)
-        group_w_out(nc.vector.tensor_copy, 0)
+        nc.scalar.copy(
+            out=w_out_grouped[:, 0:BANK, :],
+            in_=w_out_raw[:, :, 0:BANK].rearrange("p j c -> p c j"),
+        )
+        for j in range(PACK):
+            first = j % 2 * ENC_TOKENS
+            nc.scalar.activation(
+                out=sides[:, j, :, 0:T_LEN],
+                in_=enc_banks[j // 2][:, first : first + ENC_TOKENS].rearrange(
+                    "p (b t) -> p b t", b=BATCH
+                ),
+                func=IDENTITY,
+                bias=b_enc_columns[:, j : j + 1],
+            )
         quantise(nc, w_pred_grouped[:], w_pred_codes[:], w_pred_scales[:])
         pred_bank = new_bank()
         for j in range(PACK):
@@ -204,16 +239,16 @@ def tile_jointnetwork_kernel(
                 pred_bank[:, j * P : (j + 1) * P],
                 w_pred_codes, w_pred_scales, j, ENC_TOKENS, TOKENS,
             )
-        for first_j in range(0, PACK, 2):
-            nc.vector.tensor_tensor(
-                out=sides[:, first_j : first_j + 2, :, 0:T_LEN],
-                in0=enc_banks[first_j // 2][:].rearrange("p (j b t) -> p j b t", j=2, b=BATCH),
-                in1=b_enc_columns[:, first_j : first_j + 2]
-                .unsqueeze(2)
-                .unsqueeze(3)
-                .to_broadcast([P, 2, BATCH, T_LEN]),
-                op=ADD,
+        def quantise_w_out(half):
+            cols = slice(half * BANK, (half + 1) * BANK)
+            quantise(
+                nc,
+                w_out_grouped[:, cols, :].rearrange("p c j -> p (c j)"),
+                w_out_codes[:, cols],
+                w_out_scales[:, cols],
             )
+
+        quantise_w_out(0)
         nc.vector.tensor_tensor(
             out=sides[:, :, :, T_LEN : T_LEN + U_LEN],
             in0=pred_bank[:].rearrange("p (j b u) -> p j b u", j=PACK, b=BATCH),
@@ -223,7 +258,6 @@ def tile_jointnetwork_kernel(
             .to_broadcast([P, PACK, BATCH, U_LEN]),
             op=ADD,
         )
-        group_w_out(nc.scalar.copy, 1)
 
         joint_of = {}
         grouped_of = {}
@@ -233,10 +267,43 @@ def tile_jointnetwork_kernel(
         logits_of = {}
         banks_of = {}
 
-        def first_label(r, m):
-            return (r % ROUNDS_IN_BATCH) * ROW_TILES + m
+        def turn_sides(b):
+            bank = new_side_bank()
+            for j in range(PACK):
+                cols = slice(j * P, (j + 1) * P)
+                nc.tensor.transpose(bank[:, cols], sides[:, j, b, :], identity[:])
+            return bank
+
+        def keep_turned(b, bank):
+            turned_of[b] = keep.tile([P, DIM], F32, name="turned%d" % b)
+            nc.scalar.copy(out=turned_of[b][:], in_=bank[:])
+
+        def add_on_tensor(r, m):
+            adder = adders[:, added_labels.index(first_label(r, m))]
+            bank = new_side_bank()
+            for j in range(PACK):
+                cols = slice(j * P, (j + 1) * P)
+                nc.tensor.matmul(
+                    bank[:, cols],
+                    lhsT=turned_of[r // ROUNDS_IN_BATCH][:, cols],
+                    rhs=adder.rearrange("p t h -> p (t h)"),
+                    start=True,
+                    stop=True,
+                )
+            sum_of[r, m] = bank
 
         def take_tanh(r, m):
+            if r not in grouped_of:
+                grouped_of[r] = work.tile(
+                    [P, ROW_TILES, T_LEN, SLICES], BF16, align_bytes=64, name="grouped"
+                )
+            if is_added(r, m):
+                nc.scalar.activation(
+                    out=grouped_of[r][:, m].rearrange("p t (h j) -> p (t h) j", j=PACK),
+                    in_=sum_of[r, m][:].rearrange("p (j n) -> p n j", j=PACK),
+                    func=TANH,
+                )
+                return
             b = r // ROUNDS_IN_BATCH
             joint = work.tile([P, SLICES, T_LEN], BF16, align_bytes=64, name="joint%d" % m)
             for h in range(LABELS_IN_TILE):
@@ -250,48 +317,20 @@ def tile_jointnetwork_kernel(
                     )
             joint_of[r, m] = joint
 
-        def new_grouped(r):
-            if r not in grouped_of:
-                grouped_of[r] = work.tile(
-                    [P, ROW_TILES, T_LEN, SLICES], BF16, align_bytes=64, name="grouped"
-                )
-
-        def turn_sides(b):
-            bank = new_side_bank()
-            for j in range(PACK):
-                cols = slice(j * P, (j + 1) * P)
-                nc.tensor.transpose(bank[:, cols], sides[:, j, b, :], identity[:])
-            turned_of[b] = keep.tile([P, DIM], F32, name="turned%d" % b)
-            nc.scalar.copy(out=turned_of[b][:], in_=bank[:])
-
-        def add_on_tensor(r):
-            b, q = divmod(r, ROUNDS_IN_BATCH)
-            bank = new_side_bank()
-            for j in range(PACK):
-                cols = slice(j * P, (j + 1) * P)
-                nc.tensor.matmul(
-                    bank[:, cols],
-                    lhsT=turned_of[b][:, cols],
-                    rhs=adders[:, q].rearrange("p t h -> p (t h)"),
-                    start=True,
-                    stop=True,
-                )
-            sum_of[r] = bank
-
-        def take_tanh_of_sum(r):
-            new_grouped(r)
-            nc.scalar.activation(
-                out=grouped_of[r][:, ADDED_TILE].rearrange("p t (h j) -> p (t h) j", j=PACK),
-                in_=sum_of[r][:].rearrange("p (j n) -> p n j", j=PACK),
-                func=TANH,
-            )
-
         def group_joint(engine_copy, r, m):
-            new_grouped(r)
             engine_copy(
                 out=grouped_of[r][:, m].rearrange("p (c i) q -> p c q i", i=RUN),
                 in_=joint_of[r, m][:].rearrange("p q (c i) -> p c q i", i=RUN),
             )
+
+        def form_joint(r):
+            take_tanh(r, 0)
+            take_tanh(r, 1)
+            group_joint(nc.scalar.copy, r, 0)
+            take_tanh(r, 2)
+            group_joint(nc.scalar.copy, r, 1)
+            take_tanh(r, 3)
+            group_joint(nc.scalar.copy, r, 2)
 
         def quantise_joint(r, first, last):
             if r not in codes_of:
@@ -308,10 +347,11 @@ def tile_jointnetwork_kernel(
                 scales[:, cols],
             )
 
-        def multiply(r, m):
-            codes, scales = codes_of[r]
+        def multiply(tile):
+            codes, scales = codes_of[tile // ROW_TILES]
+            m = tile % ROW_TILES
             row_cols = slice(m * P, (m + 1) * P)
-            banks = []
+            banks_of[tile] = []
             for half in range(VOCAB_HALVES):
                 cols = slice(half * BANK, (half + 1) * BANK)
                 bank = new_bank()
@@ -324,101 +364,162 @@ def tile_jointnetwork_kernel(
                     start=True,
                     stop=True,
                 )
-                banks.append(bank)
-            banks_of[r, m] = banks
+                banks_of[tile].append(bank)
 
         first_sizes = [1, 1, PAIR, PAIR]
-        last_sizes = [PAIR, PAIR, PAIR, 1, PAIR, 1]
-        quads = (TILES - sum(first_sizes) - sum(last_sizes)) // ROW_TILES
+        last_sizes = [PAIR] * LAST_PAIRS
+        quads = (PLAIN_TILES - sum(first_sizes) - sum(last_sizes)) // ROW_TILES
         units = []
         for size in first_sizes + [ROW_TILES] * quads + last_sizes:
             first = units[-1][1] if units else 0
             units.append((first, first + size))
         unit_of = {i: unit for unit in units for i in range(unit[0], unit[1])}
 
-        def add_bias(i):
-            first, end = unit_of[i]
-            if i == first:
-                logits_of[first] = rows.tile(
-                    [P, end - first, VOCAB], F32, name="logits%d" % (end - first)
-                )
-            for half in range(VOCAB_HALVES):
-                cols = slice(half * BANK, (half + 1) * BANK)
-                nc.vector.tensor_tensor(
-                    out=logits_of[first][:, i - first, cols],
-                    in0=banks_of[i // ROW_TILES, i % ROW_TILES][half][:],
-                    in1=b_out_rows[:, cols],
-                    op=ADD,
-                )
-            if i == end - 1 and first < units[-VECTOR_UNITS][0]:
-                clamp_and_store(nc.gpsimd, first, end)
+        def new_logits(count):
+            logits = rows.tile(
+                [P, count, VOCAB], F32, name="logits%d" % count, bufs=LOGITS_BUFS[count]
+            )
+            return logits
 
-        def clamp_and_store(engine, first, end):
-            logits = logits_of[first]
+        def clamp(engine, out_cols, in_cols):
             engine.tensor_scalar(
-                out=logits[:],
-                in0=logits[:],
+                out=out_cols,
+                in0=in_cols,
                 scalar1=LOGIT_CLAMP,
                 scalar2=-LOGIT_CLAMP,
                 op0=MIN,
                 op1=MAX,
             )
-            for i in range(first, end, PAIR):
-                count = min(PAIR, end - i)
-                b, label = divmod(i, LABEL_STEP)
-                nc.sync.dma_start(
-                    out=out_tiles[b, :, label : label + count, :],
-                    in_=logits[:, i - first : i - first + count, :],
+
+        def add_bias(tile):
+            first, end = unit_of[tile]
+            if tile == first:
+                logits_of[first] = new_logits(end - first)
+            logits = logits_of[first]
+            for half in range(VOCAB_HALVES):
+                cols = slice(half * BANK, (half + 1) * BANK)
+                nc.vector.tensor_tensor(
+                    out=logits[:, tile - first, cols],
+                    in0=banks_of[tile][half][:],
+                    in1=b_out_rows[:, cols],
+                    op=ADD,
                 )
+            if tile == end - 1:
+                clamp(nc.gpsimd, logits[:], logits[:])
+                for i in range(first, end, PAIR):
+                    count = min(PAIR, end - i)
+                    b, label = divmod(i, LABEL_STEP)
+                    nc.sync.dma_start(
+                        out=out_tiles[b, :, label : label + count, :],
+                        in_=logits[:, i - first : i - first + count, :],
+                    )
 
-        def form_joint(r):
-            if r < VECTOR_COPY_ROUNDS:
-                for m in range(ROW_TILES):
-                    take_tanh(r, m)
-                return
-            take_tanh(r, 0)
-            take_tanh(r, 1)
-            group_joint(nc.scalar.copy, r, 0)
-            take_tanh(r, 2)
-            group_joint(nc.scalar.copy, r, 1)
-            take_tanh_of_sum(r)
-            group_joint(nc.scalar.copy, r, 2)
+        b_out_columns = keep.tile([P, VOCAB_BLOCKS], F32)
 
-        form_joint(0)
-        for half in range(VOCAB_HALVES):
-            cols = slice(half * BANK, (half + 1) * BANK)
-            quantise(
-                nc,
-                w_out_grouped[:, cols, :].rearrange("p c j -> p (c j)"),
-                w_out_codes[:, cols],
-                w_out_scales[:, cols],
+        def turn_b_out():
+            bank = new_side_bank()
+            for c in range(VOCAB_BLOCKS):
+                nc.tensor.matmul(
+                    bank[:, c : c + 1],
+                    lhsT=b_out_rows[:, c * P : (c + 1) * P],
+                    rhs=pick[:],
+                    start=True,
+                    stop=True,
+                )
+            nc.scalar.copy(out=b_out_columns[:], in_=bank[:, 0:VOCAB_BLOCKS])
+
+        last = ROUNDS - 1
+        biased = keep.tile([P, VOCAB_BLOCKS, ROUND_ROWS], F32)
+
+        def multiply_turned(c, bank):
+            codes, scales = codes_of[last]
+            nc.tensor.matmul_mx(
+                out=bank[:],
+                lhsT=w_out_codes[:, c * P : (c + 1) * P].bitcast(FP8X4),
+                lhsT_scale=w_out_scales[:, c * P : (c + 1) * P],
+                rhs=codes[:].bitcast(FP8X4),
+                rhs_scale=scales[:],
+                start=True,
+                stop=True,
             )
-        for m in range(ROW_TILES):
-            group_joint(nc.vector.tensor_copy, 0, m)
-            quantise_joint(0, m, m + 1)
-            if m < TILES_AHEAD:
-                multiply(0, m)
-        form_joint(1)
-        turn_sides(0)
-        add_on_tensor(VECTOR_COPY_ROUNDS)
+            nc.scalar.activation(
+                out=biased[:, c, :], in_=bank[:], func=IDENTITY, bias=b_out_columns[:, c : c + 1]
+            )
 
-        for r in range(ROUNDS):
-            if r + 1 < BATCH:
-                turn_sides(r + 1)
-            if r + 2 < ROUNDS:
-                form_joint(r + 2)
+        def finish_turned():
+            logits = new_logits(ROW_TILES)
+            b, first = divmod(PLAIN_TILES, LABEL_STEP)
+            for half in range(VOCAB_HALVES):
+                cols = slice(half * BANK, (half + 1) * BANK)
+                for m in range(ROW_TILES):
+                    bank = new_bank()
+                    for i in range(BLOCKS_IN_BANK):
+                        nc.tensor.transpose(
+                            bank[:, i * P : (i + 1) * P],
+                            biased[:, half * BLOCKS_IN_BANK + i, m * P : (m + 1) * P],
+                            identity[:],
+                        )
+                    clamp(nc.vector, logits[:, m, cols], bank[:])
+                    nc.sync.dma_start(
+                        out=out_tiles[b, :, first + m, cols], in_=logits[:, m, cols]
+                    )
+
+        side_bank = turn_sides(0)
+        take_tanh(0, 0)
+        take_tanh(0, 1)
+        keep_turned(0, side_bank)
+        take_tanh(0, 2)
+        take_tanh(0, 3)
+        group_joint(nc.vector.tensor_copy, 0, 0)
+        quantise_joint(0, 0, 1)
+        quantise_w_out(1)
+        multiply(0)
+        group_joint(nc.vector.tensor_copy, 0, 1)
+        quantise_joint(0, 1, 2)
+        multiply(1)
+        add_on_tensor(2, ADDED_TILE)
+        for m in range(ROW_TILES):
+            take_tanh(1, m)
+        for m in range(2):
+            add_bias(m)
+            group_joint(nc.vector.tensor_copy, 0, m + 2)
+            quantise_joint(0, m + 2, m + 3)
+            multiply(m + 2)
+        for m in range(ROW_TILES):
+            group_joint(nc.vector.tensor_copy, 1, m)
+        quantise_joint(1, 0, ROW_TILES)
+        multiply(4)
+        form_joint(2)
+        add_bias(2)
+        multiply(5)
+        add_bias(3)
+        multiply(6)
+        add_on_tensor(3, ADDED_TILE)
+
+        for r in range(1, last):
+            next_b = (r + 3) // ROUNDS_IN_BATCH
+            if (r + 3) % ROUNDS_IN_BATCH == 0 and next_b < BATCH:
+                side_bank = turn_sides(next_b)
+                keep_turned(next_b, side_bank)
+            elif r == 2:
+                turn_b_out()
+            if r == last - 1:
+                multiply_turned(0, new_side_bank())
+                multiply_turned(1, new_side_bank())
             for m in range(ROW_TILES):
                 tile = r * ROW_TILES + m
                 add_bias(tile)
-                if m == PAIR - 1 and r + 1 < ROUNDS:
-                    if r + 1 < VECTOR_COPY_ROUNDS:
-                        for n in range(ROW_TILES):
-                            group_joint(nc.vector.tensor_copy, r + 1, n)
+                if m == 1 and r + 1 < last:
                     quantise_joint(r + 1, 0, ROW_TILES)
-                if tile + TILES_AHEAD < TILES:
-                    ahead = divmod(tile + TILES_AHEAD, ROW_TILES)
-                    multiply(ahead[0], ahead[1])
+                if m == 3 and r + 2 == last:
+                    quantise_joint(last, 0, ROW_TILES)
+                if tile + TILES_AHEAD < PLAIN_TILES:
+                    multiply(tile + TILES_AHEAD)
+                if m == 1 and r < last - 1:
+                    form_joint(r + 2)
+                if r == last - 1 and m > 0:
+                    for c in (2 * m, 2 * m + 1):
+                        multiply_turned(c, new_bank())
             if r + 3 < ROUNDS:
-                add_on_tensor(r + 3)
-        for first, end in units[-VECTOR_UNITS:]:
-            clamp_and_store(nc.vector, first, end)
+                add_on_tensor(r + 3, ADDED_TILE)
+        finish_turned()

@@ -35,14 +35,12 @@ ROUNDS_IN_BATCH = LABEL_STEP // ROW_TILES
 ROUNDS = BATCH * ROUNDS_IN_BATCH
 SLICES = LABELS_IN_TILE * PACK
 PAIR = 2
-LOGITS_BUFS = {1: 2, 2: 6, 4: 3}
-LAST_PAIRS = 9
+LOGITS_BUFS = {1: 6, 2: 5, 4: 3}
+SLOTS = 3
+PAIRS_FROM = 54
+VECTOR_FROM = 62
 TILES = ROUNDS * ROW_TILES
-TILES_AHEAD = 3
 ADDED_TILE = 3
-PLAIN_TILES = TILES - ROW_TILES
-VOCAB_BLOCKS = VOCAB // P
-BLOCKS_IN_BANK = BANK // P
 RUN = 4
 
 def first_label(r, m):
@@ -70,7 +68,7 @@ def tile_jointnetwork_kernel(
         tc.tile_pool(name="keep", bufs=1) as keep,
         tc.tile_pool(name="work", bufs=3) as work,
         tc.tile_pool(name="rows", bufs=1) as rows,
-        tc.psum_pool(name="psum", bufs=2 * TILES_AHEAD) as psum,
+        tc.psum_pool(name="psum", bufs=2 * SLOTS) as psum,
         tc.psum_pool(name="side_psum", bufs=2) as side_psum,
         tc.manual_schedule(),
     ):
@@ -117,8 +115,6 @@ def tile_jointnetwork_kernel(
         warm = keep.tile([P, 1], F32)
         nc.vector.memset(warm[:], 0.0)
         nc.scalar.activation(out=warm[:], in_=warm[:], func=TANH)
-        pick = keep.tile([P, 1], BF16)
-        nc.scalar.copy(out=pick[:], in_=identity[:, 0:1])
 
         token_codes = keep.tile([P, TOKENS], U32, align_bytes=64)
         token_scales = keep.tile([P, TOKENS], U8, align_bytes=64)
@@ -366,14 +362,18 @@ def tile_jointnetwork_kernel(
                 )
                 banks_of[tile].append(bank)
 
-        first_sizes = [1, 1, PAIR, PAIR]
-        last_sizes = [PAIR] * LAST_PAIRS
-        quads = (PLAIN_TILES - sum(first_sizes) - sum(last_sizes)) // ROW_TILES
-        units = []
-        for size in first_sizes + [ROW_TILES] * quads + last_sizes:
-            first = units[-1][1] if units else 0
-            units.append((first, first + size))
-        unit_of = {i: unit for unit in units for i in range(unit[0], unit[1])}
+        def ends_unit(tile):
+            m = tile % ROW_TILES
+            return m == 1 or tile in (0, 3, 60) or (m == 3 and tile > PAIRS_FROM) or tile >= VECTOR_FROM
+
+        unit_of = {}
+        unit = []
+        for tile in range(TILES):
+            unit.append(tile)
+            if ends_unit(tile):
+                for i in unit:
+                    unit_of[i] = unit
+                unit = []
 
         def new_logits(count):
             logits = rows.tile(
@@ -392,77 +392,44 @@ def tile_jointnetwork_kernel(
             )
 
         def add_bias(tile):
-            first, end = unit_of[tile]
-            if tile == first:
-                logits_of[first] = new_logits(end - first)
-            logits = logits_of[first]
+            unit = unit_of[tile]
+            if tile == unit[0]:
+                logits_of[tile] = new_logits(len(unit))
+            logits = logits_of[unit[0]]
             for half in range(VOCAB_HALVES):
                 cols = slice(half * BANK, (half + 1) * BANK)
                 nc.vector.tensor_tensor(
-                    out=logits[:, tile - first, cols],
+                    out=logits[:, tile - unit[0], cols],
                     in0=banks_of[tile][half][:],
                     in1=b_out_rows[:, cols],
                     op=ADD,
                 )
-            if tile == end - 1:
-                clamp(nc.gpsimd, logits[:], logits[:])
-                for i in range(first, end, PAIR):
-                    count = min(PAIR, end - i)
-                    b, label = divmod(i, LABEL_STEP)
+            if tile == unit[-1]:
+                clamp(nc.vector if tile >= VECTOR_FROM else nc.gpsimd, logits[:], logits[:])
+                for i in range(0, len(unit), PAIR):
+                    count = min(PAIR, len(unit) - i)
+                    b, label = divmod(unit[i], LABEL_STEP)
                     nc.sync.dma_start(
                         out=out_tiles[b, :, label : label + count, :],
-                        in_=logits[:, i - first : i - first + count, :],
+                        in_=logits[:, i : i + count, :],
                     )
 
-        b_out_columns = keep.tile([P, VOCAB_BLOCKS], F32)
+        quantised = {}
+        written = []
+        emptied = []
 
-        def turn_b_out():
-            bank = new_side_bank()
-            for c in range(VOCAB_BLOCKS):
-                nc.tensor.matmul(
-                    bank[:, c : c + 1],
-                    lhsT=b_out_rows[:, c * P : (c + 1) * P],
-                    rhs=pick[:],
-                    start=True,
-                    stop=True,
-                )
-            nc.scalar.copy(out=b_out_columns[:], in_=bank[:, 0:VOCAB_BLOCKS])
+        def quantise_tiles(r, count):
+            done = quantised.get(r, 0)
+            quantise_joint(r, done, done + count)
+            quantised[r] = done + count
 
-        last = ROUNDS - 1
-        biased = keep.tile([P, VOCAB_BLOCKS, ROUND_ROWS], F32)
-
-        def multiply_turned(c, bank):
-            codes, scales = codes_of[last]
-            nc.tensor.matmul_mx(
-                out=bank[:],
-                lhsT=w_out_codes[:, c * P : (c + 1) * P].bitcast(FP8X4),
-                lhsT_scale=w_out_scales[:, c * P : (c + 1) * P],
-                rhs=codes[:].bitcast(FP8X4),
-                rhs_scale=scales[:],
-                start=True,
-                stop=True,
-            )
-            nc.scalar.activation(
-                out=biased[:, c, :], in_=bank[:], func=IDENTITY, bias=b_out_columns[:, c : c + 1]
-            )
-
-        def finish_turned():
-            logits = new_logits(ROW_TILES)
-            b, first = divmod(PLAIN_TILES, LABEL_STEP)
-            for half in range(VOCAB_HALVES):
-                cols = slice(half * BANK, (half + 1) * BANK)
-                for m in range(ROW_TILES):
-                    bank = new_bank()
-                    for i in range(BLOCKS_IN_BANK):
-                        nc.tensor.transpose(
-                            bank[:, i * P : (i + 1) * P],
-                            biased[:, half * BLOCKS_IN_BANK + i, m * P : (m + 1) * P],
-                            identity[:],
-                        )
-                    clamp(nc.vector, logits[:, m, cols], bank[:])
-                    nc.sync.dma_start(
-                        out=out_tiles[b, :, first + m, cols], in_=logits[:, m, cols]
-                    )
+        def write_products():
+            while len(written) < min(TILES, len(emptied) + SLOTS):
+                tile = len(written)
+                if quantised.get(tile // ROW_TILES, 0) <= tile % ROW_TILES:
+                    break
+                multiply(tile)
+                written.append(tile)
 
         side_bank = turn_sides(0)
         take_tanh(0, 0)
@@ -471,55 +438,35 @@ def tile_jointnetwork_kernel(
         take_tanh(0, 2)
         take_tanh(0, 3)
         group_joint(nc.vector.tensor_copy, 0, 0)
-        quantise_joint(0, 0, 1)
+        quantise_tiles(0, 1)
         quantise_w_out(1)
-        multiply(0)
+        write_products()
         group_joint(nc.vector.tensor_copy, 0, 1)
-        quantise_joint(0, 1, 2)
-        multiply(1)
+        quantise_tiles(0, 1)
+        write_products()
         add_on_tensor(2, ADDED_TILE)
         for m in range(ROW_TILES):
             take_tanh(1, m)
-        for m in range(2):
-            add_bias(m)
-            group_joint(nc.vector.tensor_copy, 0, m + 2)
-            quantise_joint(0, m + 2, m + 3)
-            multiply(m + 2)
-        for m in range(ROW_TILES):
-            group_joint(nc.vector.tensor_copy, 1, m)
-        quantise_joint(1, 0, ROW_TILES)
-        multiply(4)
-        form_joint(2)
-        add_bias(2)
-        multiply(5)
-        add_bias(3)
-        multiply(6)
-        add_on_tensor(3, ADDED_TILE)
 
-        for r in range(1, last):
-            next_b = (r + 3) // ROUNDS_IN_BATCH
-            if (r + 3) % ROUNDS_IN_BATCH == 0 and next_b < BATCH:
+        for r in range(ROUNDS):
+            if r > 0 and (r + 3) % ROUNDS_IN_BATCH == 0 and r + 3 < ROUNDS:
+                next_b = (r + 3) // ROUNDS_IN_BATCH
                 side_bank = turn_sides(next_b)
                 keep_turned(next_b, side_bank)
-            elif r == 2:
-                turn_b_out()
-            if r == last - 1:
-                multiply_turned(0, new_side_bank())
-                multiply_turned(1, new_side_bank())
             for m in range(ROW_TILES):
                 tile = r * ROW_TILES + m
                 add_bias(tile)
-                if m == 1 and r + 1 < last:
-                    quantise_joint(r + 1, 0, ROW_TILES)
-                if m == 3 and r + 2 == last:
-                    quantise_joint(last, 0, ROW_TILES)
-                if tile + TILES_AHEAD < PLAIN_TILES:
-                    multiply(tile + TILES_AHEAD)
-                if m == 1 and r < last - 1:
+                emptied.append(tile)
+                if r == 0 and m < 2:
+                    group_joint(nc.vector.tensor_copy, 0, m + 2)
+                    quantise_tiles(0, 1)
+                if m == 1 and r + 1 < ROUNDS:
+                    if r == 0:
+                        for n in range(ROW_TILES):
+                            group_joint(nc.vector.tensor_copy, 1, n)
+                    quantise_tiles(r + 1, ROW_TILES)
+                write_products()
+                if m == 1 and r + 2 < ROUNDS:
                     form_joint(r + 2)
-                if r == last - 1 and m > 0:
-                    for c in (2 * m, 2 * m + 1):
-                        multiply_turned(c, new_bank())
             if r + 3 < ROUNDS:
                 add_on_tensor(r + 3, ADDED_TILE)
-        finish_turned()

@@ -11,7 +11,6 @@ MULT = mybir.AluOpType.mult
 MIN = mybir.AluOpType.min
 MAX = mybir.AluOpType.max
 TANH = mybir.ActivationFunctionType.Tanh
-IDENTITY = mybir.ActivationFunctionType.Identity
 
 P = 128
 PACK = 4
@@ -35,7 +34,7 @@ ROUNDS_IN_BATCH = LABEL_STEP // ROW_TILES
 ROUNDS = BATCH * ROUNDS_IN_BATCH
 SLICES = LABELS_IN_TILE * PACK
 PAIR = 2
-LOGITS_BUFS = {1: 6, 2: 5, 4: 3}
+LOGITS_BUFS = {1: 4, 2: 4, 4: 4}
 SLOTS = 3
 PAIRS_FROM = 54
 VECTOR_FROM = 62
@@ -48,7 +47,7 @@ def first_label(r, m):
 
 
 def is_added(r, m):
-    return m == ADDED_TILE and r >= 2
+    return (m == ADDED_TILE and r >= 2) or (r == 1 and m >= 2)
 
 
 FLOPS = 2 * DIM * (ENC_TOKENS * DIM + PRED_TOKENS * DIM + BATCH * T_LEN * U_LEN * VOCAB)
@@ -82,20 +81,20 @@ def tile_jointnetwork_kernel(
             return bank
 
         tokens = keep.tile([P, TOKEN_TILES, DIM], BF16)
-        nc.sync.dma_start(
-            out=tokens[:, 0:2, :],
-            in_=encoder_out.flatten_outer_dims().rearrange("(n p) k -> p n k", p=P),
-        )
         raw_of = {}
-        for name, weight, width in (("w_enc", W_enc, DIM), ("w_pred", W_pred, DIM)):
-            raw_of[name] = keep.tile([P, PACK, width], BF16, name=name + "_raw")
+        for name, weight, first, rows_in in (
+            ("w_enc", W_enc, 0, encoder_out),
+            ("w_pred", W_pred, 2, predictor_out),
+        ):
+            raw_of[name] = keep.tile([P, PACK, DIM], BF16, name=name + "_raw")
             nc.sync.dma_start(
                 out=raw_of[name][:], in_=weight.rearrange("(p j) c -> p j c", j=PACK)
             )
-            if name == "w_enc":
-                nc.sync.dma_start(
-                    out=tokens[:, 2, :], in_=predictor_out.flatten_outer_dims()
-                )
+            flat = rows_in.flatten_outer_dims()
+            nc.sync.dma_start(
+                out=tokens[:, first : first + flat.shape[0] // P, :],
+                in_=flat.rearrange("(n p) k -> p n k", p=P),
+            )
         w_out_raw = keep.tile([P, PACK, VOCAB], BF16)
         for half in range(VOCAB_HALVES):
             cols = slice(half * BANK, (half + 1) * BANK)
@@ -142,13 +141,11 @@ def tile_jointnetwork_kernel(
                 op=ADD,
             )
 
-        def group_projection(engine_copy, raw, name):
-            grouped = keep.tile([P, DIM * PACK], BF16, align_bytes=64, name=name)
+        def group_projection(engine_copy, raw, grouped, first, end):
             engine_copy(
-                out=grouped[:].rearrange("p (t m j) -> p t m j", t=PACK, j=PACK),
-                in_=raw[:].rearrange("p j (m t) -> p t m j", t=PACK),
+                out=grouped[:].rearrange("p (t m j) -> p t m j", t=PACK, j=PACK)[:, first:end],
+                in_=raw[:].rearrange("p j (m t) -> p t m j", t=PACK)[:, first:end],
             )
-            return grouped
 
         token_grouped = keep.tile([P, TOKENS * PACK], BF16, align_bytes=64)
 
@@ -183,13 +180,16 @@ def tile_jointnetwork_kernel(
                 stop=True,
             )
 
-        w_enc_grouped = group_projection(nc.vector.tensor_copy, raw_of["w_enc"], "w_enc_grouped")
+        w_enc_grouped = keep.tile([P, DIM * PACK], BF16, align_bytes=64)
+        w_pred_grouped = keep.tile([P, DIM * PACK], BF16, align_bytes=64)
+        group_projection(nc.vector.tensor_copy, raw_of["w_enc"], w_enc_grouped, 0, PACK)
         group_tokens(0)
         group_tokens(1)
-        group_tokens(2)
-        quantise_tokens(0, ENC_TOKENS)
         quantise(nc, w_enc_grouped[:], w_enc_codes[:], w_enc_scales[:])
-        w_pred_grouped = group_projection(nc.vector.tensor_copy, raw_of["w_pred"], "w_pred_grouped")
+        quantise_tokens(0, ENC_TOKENS)
+        group_projection(nc.vector.tensor_copy, raw_of["w_pred"], w_pred_grouped, 0, 2)
+        group_projection(nc.scalar.copy, raw_of["w_pred"], w_pred_grouped, 2, PACK)
+        group_tokens(2)
         quantise_tokens(ENC_TOKENS, TOKENS)
 
         w_out_grouped = keep.tile([P, VOCAB, PACK], BF16, align_bytes=64)
@@ -218,16 +218,6 @@ def tile_jointnetwork_kernel(
             out=w_out_grouped[:, 0:BANK, :],
             in_=w_out_raw[:, :, 0:BANK].rearrange("p j c -> p c j"),
         )
-        for j in range(PACK):
-            first = j % 2 * ENC_TOKENS
-            nc.scalar.activation(
-                out=sides[:, j, :, 0:T_LEN],
-                in_=enc_banks[j // 2][:, first : first + ENC_TOKENS].rearrange(
-                    "p (b t) -> p b t", b=BATCH
-                ),
-                func=IDENTITY,
-                bias=b_enc_columns[:, j : j + 1],
-            )
         quantise(nc, w_pred_grouped[:], w_pred_codes[:], w_pred_scales[:])
         pred_bank = new_bank()
         for j in range(PACK):
@@ -244,7 +234,16 @@ def tile_jointnetwork_kernel(
                 w_out_scales[:, cols],
             )
 
-        quantise_w_out(0)
+        for first_j in range(0, PACK, 2):
+            nc.vector.tensor_tensor(
+                out=sides[:, first_j : first_j + 2, :, 0:T_LEN],
+                in0=enc_banks[first_j // 2][:].rearrange("p (j b t) -> p j b t", j=2, b=BATCH),
+                in1=b_enc_columns[:, first_j : first_j + 2]
+                .unsqueeze(2)
+                .unsqueeze(3)
+                .to_broadcast([P, 2, BATCH, T_LEN]),
+                op=ADD,
+            )
         nc.vector.tensor_tensor(
             out=sides[:, :, :, T_LEN : T_LEN + U_LEN],
             in0=pred_bank[:].rearrange("p (j b u) -> p j b u", j=PACK, b=BATCH),
@@ -431,6 +430,7 @@ def tile_jointnetwork_kernel(
                 multiply(tile)
                 written.append(tile)
 
+        quantise_w_out(0)
         side_bank = turn_sides(0)
         take_tanh(0, 0)
         take_tanh(0, 1)
@@ -444,15 +444,16 @@ def tile_jointnetwork_kernel(
         group_joint(nc.vector.tensor_copy, 0, 1)
         quantise_tiles(0, 1)
         write_products()
-        add_on_tensor(2, ADDED_TILE)
+        add_on_tensor(1, 2)
+        add_on_tensor(1, 3)
         for m in range(ROW_TILES):
             take_tanh(1, m)
 
         for r in range(ROUNDS):
-            if r > 0 and (r + 3) % ROUNDS_IN_BATCH == 0 and r + 3 < ROUNDS:
-                next_b = (r + 3) // ROUNDS_IN_BATCH
+            next_b = r // ROUNDS_IN_BATCH + 1
+            turns_next_b = r % ROUNDS_IN_BATCH == 0 and next_b < BATCH
+            if turns_next_b:
                 side_bank = turn_sides(next_b)
-                keep_turned(next_b, side_bank)
             for m in range(ROW_TILES):
                 tile = r * ROW_TILES + m
                 add_bias(tile)
@@ -462,11 +463,15 @@ def tile_jointnetwork_kernel(
                     quantise_tiles(0, 1)
                 if m == 1 and r + 1 < ROUNDS:
                     if r == 0:
-                        for n in range(ROW_TILES):
-                            group_joint(nc.vector.tensor_copy, 1, n)
+                        group_joint(nc.vector.tensor_copy, 1, 0)
+                        group_joint(nc.vector.tensor_copy, 1, 1)
                     quantise_tiles(r + 1, ROW_TILES)
                 write_products()
                 if m == 1 and r + 2 < ROUNDS:
+                    if r == 0:
+                        add_on_tensor(2, ADDED_TILE)
                     form_joint(r + 2)
+                    if turns_next_b:
+                        keep_turned(next_b, side_bank)
             if r + 3 < ROUNDS:
                 add_on_tensor(r + 3, ADDED_TILE)

import concourse.mybir as mybir
from concourse.masks import make_identity

F32 = mybir.dt.float32
BF16 = mybir.dt.bfloat16
U32 = mybir.dt.uint32
U8 = mybir.dt.uint8
FP8X4 = mybir.dt.float8_e4m3fn_x4
ADD = mybir.AluOpType.add
MULT = mybir.AluOpType.mult
MIN = mybir.AluOpType.min
MAX = mybir.AluOpType.max
TANH = mybir.ActivationFunctionType.Tanh

P = 128
PACK = 4
BATCH, T_LEN, U_LEN = 4, 64, 32
DIM = P * PACK
VOCAB = 1024
BANK = 512
VOCAB_HALVES = VOCAB // BANK
LOGIT_CLAMP = 15.0

ENC_TOKENS = BATCH * T_LEN
PRED_TOKENS = BATCH * U_LEN
TOKENS = ENC_TOKENS + PRED_TOKENS
TOKEN_TILES = TOKENS // P

LABELS_IN_TILE = 2
LABEL_STEP = U_LEN // LABELS_IN_TILE
ROW_TILES = 4
ROUND_ROWS = ROW_TILES * P
ROUNDS_IN_BATCH = LABEL_STEP // ROW_TILES
ROUNDS = BATCH * ROUNDS_IN_BATCH
SLICES = LABELS_IN_TILE * PACK
PAIR = 2
LOGITS_BUFS = {1: 4, 2: 4, 4: 4}
SLOTS = 3
PAIRS_FROM = 54
VECTOR_FROM = 62
TILES = ROUNDS * ROW_TILES
ADDED_TILE = 3
RUN = 4

def first_label(r, m):
    return (r % ROUNDS_IN_BATCH) * ROW_TILES + m


def is_added(r, m):
    return (m == ADDED_TILE and r >= 2) or (r == 1 and m >= 2)


FLOPS = 2 * DIM * (ENC_TOKENS * DIM + PRED_TOKENS * DIM + BATCH * T_LEN * U_LEN * VOCAB)


def quantise(nc, grouped, codes, scales):
    nc.vector.quantize_mx(out=codes.bitcast(FP8X4), scales=scales, in_=grouped)


def tile_jointnetwork_kernel(
    tc, encoder_out, predictor_out, W_enc, b_enc, W_pred, b_pred, W_out, b_out, out
):
    nc = tc.nc
    out_tiles = out.rearrange("b t (h u) v -> b (t h) u v", h=LABELS_IN_TILE)

    with (
        tc.tile_pool(name="keep", bufs=1) as keep,
        tc.tile_pool(name="work", bufs=3) as work,
        tc.tile_pool(name="rows", bufs=1) as rows,
        tc.psum_pool(name="psum", bufs=2 * SLOTS) as psum,
        tc.psum_pool(name="side_psum", bufs=2) as side_psum,
        tc.manual_schedule(),
    ):

        def new_bank():
            bank = psum.tile([P, BANK], F32, name="bank")
            return bank

        def new_side_bank():
            bank = side_psum.tile([P, BANK], F32, name="side_bank")
            return bank

        tokens = keep.tile([P, TOKEN_TILES, DIM], BF16)
        raw_of = {}
        for name, weight, first, rows_in in (
            ("w_enc", W_enc, 0, encoder_out),
            ("w_pred", W_pred, 2, predictor_out),
        ):
            raw_of[name] = keep.tile([P, PACK, DIM], BF16, name=name + "_raw")
            nc.sync.dma_start(
                out=raw_of[name][:], in_=weight.rearrange("(p j) c -> p j c", j=PACK)
            )
            flat = rows_in.flatten_outer_dims()
            nc.sync.dma_start(
                out=tokens[:, first : first + flat.shape[0] // P, :],
                in_=flat.rearrange("(n p) k -> p n k", p=P),
            )
        w_out_raw = keep.tile([P, PACK, VOCAB], BF16)
        for half in range(VOCAB_HALVES):
            cols = slice(half * BANK, (half + 1) * BANK)
            nc.sync.dma_start(
                out=w_out_raw[:, :, cols],
                in_=W_out[:, cols].rearrange("(p j) c -> p j c", j=PACK),
            )
        b_out_rows = keep.tile([P, VOCAB], BF16)
        nc.sync.dma_start(out=b_out_rows[:], in_=b_out.partition_broadcast(P))
        b_enc_columns = keep.tile([P, PACK], BF16)
        nc.scalar.dma_start(out=b_enc_columns[:], in_=b_enc.rearrange("(p j) -> p j", j=PACK))
        b_pred_columns = keep.tile([P, PACK], BF16)
        nc.scalar.dma_start(out=b_pred_columns[:], in_=b_pred.rearrange("(p j) -> p j", j=PACK))

        identity = keep.tile([P, P], F32)
        make_identity(nc, identity[:])
        warm = keep.tile([P, 1], F32)
        nc.vector.memset(warm[:], 0.0)
        nc.scalar.activation(out=warm[:], in_=warm[:], func=TANH)

        token_codes = keep.tile([P, TOKENS], U32, align_bytes=64)
        token_scales = keep.tile([P, TOKENS], U8, align_bytes=64)
        w_enc_codes = keep.tile([P, DIM], U32, align_bytes=64)
        w_enc_scales = keep.tile([P, DIM], U8, align_bytes=64)
        w_pred_codes = keep.tile([P, DIM], U32, align_bytes=64)
        w_pred_scales = keep.tile([P, DIM], U8, align_bytes=64)
        w_out_codes = keep.tile([P, VOCAB], U32, align_bytes=64)
        w_out_scales = keep.tile([P, VOCAB], U8, align_bytes=64)
        sides = keep.tile([P, PACK, BATCH, P], F32)
        nc.gpsimd.memset(sides[:, :, :, T_LEN + U_LEN :], 0.0)
        added_labels = sorted(
            {first_label(r, m) for r in range(ROUNDS) for m in range(ROW_TILES) if is_added(r, m)}
        )
        adders = keep.tile([P, len(added_labels), T_LEN, LABELS_IN_TILE], F32)
        for a, first in enumerate(added_labels):
            label = T_LEN + first
            shape = [P, T_LEN, LABELS_IN_TILE]
            nc.gpsimd.tensor_tensor(
                out=adders[:, a],
                in0=identity[:, 0:T_LEN].unsqueeze(2).to_broadcast(shape),
                in1=identity[:, label : label + LABEL_STEP + 1 : LABEL_STEP]
                .unsqueeze(1)
                .to_broadcast(shape),
                op=ADD,
            )

        def group_projection(engine_copy, raw, grouped, first, end):
            engine_copy(
                out=grouped[:].rearrange("p (t m j) -> p t m j", t=PACK, j=PACK)[:, first:end],
                in_=raw[:].rearrange("p j (m t) -> p t m j", t=PACK)[:, first:end],
            )

        token_grouped = keep.tile([P, TOKENS * PACK], BF16, align_bytes=64)

        def group_tokens(n):
            flipped = new_side_bank()
            words = tokens[:, n, :].bitcast(F32)
            for w in range(2):
                nc.tensor.transpose(flipped[:, w * P : (w + 1) * P], words[:, w::2], identity[:])
            nc.scalar.copy(
                out=token_grouped[:, n * P * PACK : (n + 1) * P * PACK]
                .bitcast(F32)
                .rearrange("p (r w) -> p r w", w=2),
                in_=flipped[:, 0 : 2 * P].rearrange("p (w r) -> p r w", w=2),
            )

        def quantise_tokens(first, last):
            quantise(
                nc,
                token_grouped[:, first * PACK : last * PACK],
                token_codes[:, first:last],
                token_scales[:, first:last],
            )

        def project(out_cols, codes, scales, j, first, last):
            nc.tensor.matmul_mx(
                out=out_cols,
                lhsT=codes[:, j * P : (j + 1) * P].bitcast(FP8X4),
                lhsT_scale=scales[:, j * P : (j + 1) * P],
                rhs=token_codes[:, first:last].bitcast(FP8X4),
                rhs_scale=token_scales[:, first:last],
                start=True,
                stop=True,
            )

        w_enc_grouped = keep.tile([P, DIM * PACK], BF16, align_bytes=64)
        w_pred_grouped = keep.tile([P, DIM * PACK], BF16, align_bytes=64)
        group_projection(nc.vector.tensor_copy, raw_of["w_enc"], w_enc_grouped, 0, PACK)
        group_tokens(0)
        group_tokens(1)
        quantise(nc, w_enc_grouped[:], w_enc_codes[:], w_enc_scales[:])
        quantise_tokens(0, ENC_TOKENS)
        group_projection(nc.vector.tensor_copy, raw_of["w_pred"], w_pred_grouped, 0, 2)
        group_projection(nc.scalar.copy, raw_of["w_pred"], w_pred_grouped, 2, PACK)
        group_tokens(2)
        quantise_tokens(ENC_TOKENS, TOKENS)

        w_out_grouped = keep.tile([P, VOCAB, PACK], BF16, align_bytes=64)

        for first in range(BANK, VOCAB, P):
            cols = slice(first, first + P)
            nc.gpsimd.tensor_scalar(
                out=w_out_grouped[:, cols, :],
                in0=w_out_raw[:, :, cols].rearrange("p j c -> p c j"),
                scalar1=1.0,
                scalar2=0.0,
                op0=MULT,
                op1=ADD,
            )

        enc_banks = []
        for first_j in range(0, PACK, 2):
            bank = new_bank()
            for j in range(first_j, first_j + 2):
                project(
                    bank[:, (j - first_j) * ENC_TOKENS : (j - first_j + 1) * ENC_TOKENS],
                    w_enc_codes, w_enc_scales, j, 0, ENC_TOKENS,
                )
            enc_banks.append(bank)
        nc.scalar.copy(
            out=w_out_grouped[:, 0:BANK, :],
            in_=w_out_raw[:, :, 0:BANK].rearrange("p j c -> p c j"),
        )
        quantise(nc, w_pred_grouped[:], w_pred_codes[:], w_pred_scales[:])
        pred_bank = new_bank()
        for j in range(PACK):
            project(
                pred_bank[:, j * P : (j + 1) * P],
                w_pred_codes, w_pred_scales, j, ENC_TOKENS, TOKENS,
            )
        def quantise_w_out(half):
            cols = slice(half * BANK, (half + 1) * BANK)
            quantise(
                nc,
                w_out_grouped[:, cols, :].rearrange("p c j -> p (c j)"),
                w_out_codes[:, cols],
                w_out_scales[:, cols],
            )

        for first_j in range(0, PACK, 2):
            nc.vector.tensor_tensor(
                out=sides[:, first_j : first_j + 2, :, 0:T_LEN],
                in0=enc_banks[first_j // 2][:].rearrange("p (j b t) -> p j b t", j=2, b=BATCH),
                in1=b_enc_columns[:, first_j : first_j + 2]
                .unsqueeze(2)
                .unsqueeze(3)
                .to_broadcast([P, 2, BATCH, T_LEN]),
                op=ADD,
            )
        nc.vector.tensor_tensor(
            out=sides[:, :, :, T_LEN : T_LEN + U_LEN],
            in0=pred_bank[:].rearrange("p (j b u) -> p j b u", j=PACK, b=BATCH),
            in1=b_pred_columns[:]
            .unsqueeze(2)
            .unsqueeze(3)
            .to_broadcast([P, PACK, BATCH, U_LEN]),
            op=ADD,
        )

        joint_of = {}
        grouped_of = {}
        turned_of = {}
        sum_of = {}
        codes_of = {}
        logits_of = {}
        banks_of = {}

        def turn_sides(b):
            bank = new_side_bank()
            for j in range(PACK):
                cols = slice(j * P, (j + 1) * P)
                nc.tensor.transpose(bank[:, cols], sides[:, j, b, :], identity[:])
            return bank

        def keep_turned(b, bank):
            turned_of[b] = keep.tile([P, DIM], F32, name="turned%d" % b)
            nc.scalar.copy(out=turned_of[b][:], in_=bank[:])

        def add_on_tensor(r, m):
            adder = adders[:, added_labels.index(first_label(r, m))]
            bank = new_side_bank()
            for j in range(PACK):
                cols = slice(j * P, (j + 1) * P)
                nc.tensor.matmul(
                    bank[:, cols],
                    lhsT=turned_of[r // ROUNDS_IN_BATCH][:, cols],
                    rhs=adder.rearrange("p t h -> p (t h)"),
                    start=True,
                    stop=True,
                )
            sum_of[r, m] = bank

        def take_tanh(r, m):
            if r not in grouped_of:
                grouped_of[r] = work.tile(
                    [P, ROW_TILES, T_LEN, SLICES], BF16, align_bytes=64, name="grouped"
                )
            if is_added(r, m):
                nc.scalar.activation(
                    out=grouped_of[r][:, m].rearrange("p t (h j) -> p (t h) j", j=PACK),
                    in_=sum_of[r, m][:].rearrange("p (j n) -> p n j", j=PACK),
                    func=TANH,
                )
                return
            b = r // ROUNDS_IN_BATCH
            joint = work.tile([P, SLICES, T_LEN], BF16, align_bytes=64, name="joint%d" % m)
            for h in range(LABELS_IN_TILE):
                label = T_LEN + first_label(r, m) + h * LABEL_STEP
                for j in range(PACK):
                    nc.scalar.activation(
                        out=joint[:, h * PACK + j, :],
                        in_=sides[:, j, b, 0:T_LEN],
                        func=TANH,
                        bias=sides[:, j, b, label : label + 1],
                    )
            joint_of[r, m] = joint

        def group_joint(engine_copy, r, m):
            engine_copy(
                out=grouped_of[r][:, m].rearrange("p (c i) q -> p c q i", i=RUN),
                in_=joint_of[r, m][:].rearrange("p q (c i) -> p c q i", i=RUN),
            )

        def form_joint(r):
            take_tanh(r, 0)
            take_tanh(r, 1)
            group_joint(nc.scalar.copy, r, 0)
            take_tanh(r, 2)
            group_joint(nc.scalar.copy, r, 1)
            take_tanh(r, 3)
            group_joint(nc.scalar.copy, r, 2)

        def quantise_joint(r, first, last):
            if r not in codes_of:
                codes_of[r] = (
                    work.tile([P, ROUND_ROWS], U32, align_bytes=64, name="joint_codes"),
                    work.tile([P, ROUND_ROWS], U8, align_bytes=64, name="joint_scales"),
                )
            codes, scales = codes_of[r]
            cols = slice(first * P, last * P)
            quantise(
                nc,
                grouped_of[r][:, first:last].rearrange("p m t q -> p (m t q)"),
                codes[:, cols],
                scales[:, cols],
            )

        def multiply(tile):
            codes, scales = codes_of[tile // ROW_TILES]
            m = tile % ROW_TILES
            row_cols = slice(m * P, (m + 1) * P)
            banks_of[tile] = []
            for half in range(VOCAB_HALVES):
                cols = slice(half * BANK, (half + 1) * BANK)
                bank = new_bank()
                nc.tensor.matmul_mx(
                    out=bank[:],
                    lhsT=codes[:, row_cols].bitcast(FP8X4),
                    lhsT_scale=scales[:, row_cols],
                    rhs=w_out_codes[:, cols].bitcast(FP8X4),
                    rhs_scale=w_out_scales[:, cols],
                    start=True,
                    stop=True,
                )
                banks_of[tile].append(bank)

        def ends_unit(tile):
            m = tile % ROW_TILES
            return m == 1 or tile in (0, 3, 60) or (m == 3 and tile > PAIRS_FROM) or tile >= VECTOR_FROM

        unit_of = {}
        unit = []
        for tile in range(TILES):
            unit.append(tile)
            if ends_unit(tile):
                for i in unit:
                    unit_of[i] = unit
                unit = []

        def new_logits(count):
            logits = rows.tile(
                [P, count, VOCAB], F32, name="logits%d" % count, bufs=LOGITS_BUFS[count]
            )
            return logits

        def clamp(engine, out_cols, in_cols):
            engine.tensor_scalar(
                out=out_cols,
                in0=in_cols,
                scalar1=LOGIT_CLAMP,
                scalar2=-LOGIT_CLAMP,
                op0=MIN,
                op1=MAX,
            )

        def add_bias(tile):
            unit = unit_of[tile]
            if tile == unit[0]:
                logits_of[tile] = new_logits(len(unit))
            logits = logits_of[unit[0]]
            for half in range(VOCAB_HALVES):
                cols = slice(half * BANK, (half + 1) * BANK)
                nc.vector.tensor_tensor(
                    out=logits[:, tile - unit[0], cols],
                    in0=banks_of[tile][half][:],
                    in1=b_out_rows[:, cols],
                    op=ADD,
                )
            if tile == unit[-1]:
                clamp(nc.vector if tile >= VECTOR_FROM else nc.gpsimd, logits[:], logits[:])
                for i in range(0, len(unit), PAIR):
                    count = min(PAIR, len(unit) - i)
                    b, label = divmod(unit[i], LABEL_STEP)
                    nc.sync.dma_start(
                        out=out_tiles[b, :, label : label + count, :],
                        in_=logits[:, i : i + count, :],
                    )

        quantised = {}
        written = []
        emptied = []

        def quantise_tiles(r, count):
            done = quantised.get(r, 0)
            quantise_joint(r, done, done + count)
            quantised[r] = done + count

        def write_products():
            while len(written) < min(TILES, len(emptied) + SLOTS):
                tile = len(written)
                if quantised.get(tile // ROW_TILES, 0) <= tile % ROW_TILES:
                    break
                multiply(tile)
                written.append(tile)

        quantise_w_out(0)
        side_bank = turn_sides(0)
        take_tanh(0, 0)
        take_tanh(0, 1)
        keep_turned(0, side_bank)
        take_tanh(0, 2)
        take_tanh(0, 3)
        group_joint(nc.vector.tensor_copy, 0, 0)
        quantise_tiles(0, 1)
        quantise_w_out(1)
        write_products()
        group_joint(nc.vector.tensor_copy, 0, 1)
        quantise_tiles(0, 1)
        write_products()
        add_on_tensor(1, 2)
        add_on_tensor(1, 3)
        for m in range(ROW_TILES):
            take_tanh(1, m)

        for r in range(ROUNDS):
            next_b = r // ROUNDS_IN_BATCH + 1
            turns_next_b = r % ROUNDS_IN_BATCH == 0 and next_b < BATCH
            if turns_next_b:
                side_bank = turn_sides(next_b)
            for m in range(ROW_TILES):
                tile = r * ROW_TILES + m
                add_bias(tile)
                emptied.append(tile)
                if r == 0 and m < 2:
                    group_joint(nc.vector.tensor_copy, 0, m + 2)
                    quantise_tiles(0, 1)
                if m == 1 and r + 1 < ROUNDS:
                    if r == 0:
                        group_joint(nc.vector.tensor_copy, 1, 0)
                        group_joint(nc.vector.tensor_copy, 1, 1)
                    quantise_tiles(r + 1, ROW_TILES)
                write_products()
                if m == 1 and r + 2 < ROUNDS:
                    if r == 0:
                        add_on_tensor(2, ADDED_TILE)
                    form_joint(r + 2)
                    if turns_next_b:
                        keep_turned(next_b, side_bank)
            if r + 3 < ROUNDS:
                add_on_tensor(r + 3, ADDED_TILE)
